import numpy as np
import ml_dtypes


def mxq(x, axis, fmt="e4m3"):
    dtype, down = {"e4m3": (ml_dtypes.float8_e4m3fn, 7), "e5m2": (ml_dtypes.float8_e5m2, 14)}[fmt]
    v = np.moveaxis(np.asarray(x, np.float32).astype(ml_dtypes.bfloat16).astype(np.float64), axis, -1)
    blocks = v.reshape(v.shape[:-1] + (-1, 32))
    amax = np.abs(blocks).max(-1, keepdims=True)
    byte = np.maximum(np.where(amax > 0, np.frexp(amax)[1] - 1 + 127, 0) - down, 1)
    scale = np.exp2(byte - 127.0)
    codes = (blocks / scale).astype(np.float32).astype(dtype).astype(np.float64)
    return np.moveaxis((codes * scale).reshape(v.shape), -1, axis)


WIDE = False


def mx_kscale(k):
    if not WIDE:
        return np.ones(k)
    levels = np.array([20, -20, 10, -10, 0])
    a = np.random.permutation(np.resize(levels, k // 512 * 4)).reshape(k // 512, 4)
    idx = np.arange(k)
    return np.exp2(a[idx // 512, idx % 128 // 32])


BF16 = ml_dtypes.bfloat16


def bf(x):
    return np.asarray(x, np.float32).astype(BF16)


def f64(x):
    return np.asarray(x).astype(np.float64)


B, CI, CO, OH, OW, K = 2048, 32, 512, 2, 2, 4
STRIDE = 1
IH, IW = (OH - 1) * STRIDE + K, (OW - 1) * STRIDE + K
P = OH * OW
KC = CI * K * K


def setup_inputs():
    u = mx_kscale(CO)
    x = np.random.uniform(0.0, 1.0, (B, CI, IH, IW))
    w = np.random.standard_normal((OH, OW, CI, K, K, CO)) * 1.5 / np.sqrt(KC) / u[None, None, None, None, None, :]
    g = (np.random.standard_normal((B, CO, OH, OW)) * np.exp2(np.random.randint(-12, 1, (B, 1, OH, OW))) * 4.0
         * u[None, :, None, None])
    return {"in_spikes": bf(x), "weights": bf(w), "grad_out": bf(g)}


def reference(in_spikes, weights, grad_out):
    g = f64(grad_out).reshape(B, CO, P).transpose(2, 0, 1)
    w = f64(weights).reshape(P, KC, CO)
    d = mxq(g, 2, "e5m2") @ mxq(w, 2, "e4m3").transpose(0, 2, 1)
    d = d.reshape(OH, OW, B, CI, K, K)
    out = np.zeros((B, CI, IH, IW))
    for i in range(OH):
        for j in range(OW):
            out[:, :, i:i + K, j:j + K] += d[i, j]
    return out

@@ -1,0 +1,188 @@
+from contextlib import ExitStack
+
+import concourse.mybir as mybir
+from concourse.masks import make_identity
+
+F32 = mybir.dt.float32
+BF16 = mybir.dt.bfloat16
+U32 = mybir.dt.uint32
+U8 = mybir.dt.uint8
+I32 = mybir.dt.int32
+E5X4 = mybir.dt.float8_e5m2_x4
+E4X4 = mybir.dt.float8_e4m3fn_x4
+
+P = 128
+B, CI, CO, OH, OW, KW = 2048, 32, 512, 2, 2, 4
+IH, IW = 5, 5
+NPOS = OH * OW
+NT = B // P
+GROUP = 2
+NG = NT // GROUP
+OUTC = CI * IH * IW
+NB = 512
+
+FLOPS = 2 * NPOS * B * CO * CI * KW * KW
+BYTES = 2 * B * CO * NPOS + 2 * NPOS * CI * KW * KW * CO + 4 * B * OUTC
+
+PIN = False
+
+
+def tile_stdpconvinhibit_t_kernel(tc, in_spikes, weights, grad_out, out):
+    nc = tc.nc
+    g_view = grad_out.rearrange("(q n) k i j -> q n (k i j)", n=NT)
+    o_view = out.rearrange("(q n) c h w -> q n (c h w)", n=NT)
+    w_view = weights.rearrange("i j c u v k -> (i j c u v) k").rearrange("(n q) k -> q n k", q=P)
+
+    with ExitStack() as ctx:
+        const = ctx.enter_context(tc.tile_pool(name="const", bufs=1))
+        graw_pool = ctx.enter_context(tc.tile_pool(name="graw", bufs=NG))
+        gd_pool = ctx.enter_context(tc.tile_pool(name="gd", bufs=4))
+        ggrp_pool = ctx.enter_context(tc.tile_pool(name="ggrp", bufs=4))
+        gq_pool = ctx.enter_context(tc.tile_pool(name="gq", bufs=6))
+        acc_pool = ctx.enter_context(tc.tile_pool(name="acc", bufs=3))
+        psum_t = ctx.enter_context(tc.psum_pool(name="psum_t", bufs=4))
+        psum_m = ctx.enter_context(tc.psum_pool(name="psum_m", bufs=4))
+        if PIN:
+            ctx.enter_context(tc.manual_schedule())
+
+        ident = const.tile([P, P], F32, name="ident")
+        make_identity(nc, ident[:])
+
+        wraw = [const.tile([P, 4 * CO], BF16, name="wraw%d" % p) for p in range(NPOS)]
+        wgrp = [const.tile([P, 2 * NB * 4], BF16, name="wgrp%d" % p, align_bytes=64) for p in range(NPOS)]
+        wcod = [const.tile([P, 2 * NB], U32, name="wcod%d" % p, align_bytes=64) for p in range(NPOS)]
+        wsca = [const.tile([P, 2 * NB], U8, name="wsca%d" % p, align_bytes=64) for p in range(NPOS)]
+        for p in range(NPOS):
+            nc.vector.memset(wgrp[p][:].bitcast(I32), 0)
+
+        graw = {}
+        gd = {}
+        gt = {}
+        gq = {}
+
+        def load_g(s):
+            t = graw_pool.tile([P, GROUP * 4 * CO], BF16, name="graw")
+            nc.sync.dma_start(
+                out=t[:].rearrange("q (n e) -> q n e", n=GROUP),
+                in_=g_view[:, GROUP * s : GROUP * (s + 1), :],
+            )
+            graw[s] = t
+
+        def load_w(p):
+            nc.sync.dma_start(
+                out=wraw[p][:].rearrange("q (n k) -> q n k", n=4),
+                in_=w_view[:, 4 * p : 4 * (p + 1), :],
+            )
+
+        def prep_w(p):
+            i, j = p // OW, p % OW
+            words = wraw[p][:].bitcast(F32)
+            dst = wgrp[p][:].bitcast(F32)[:, 0 : OUTC * 2].rearrange(
+                "q (c y x u) -> q c y x u", c=CI, y=IH, x=IW, u=2
+            )
+            for h in range(2):
+                wt = psum_m.tile([P, NB], F32, name="mx")
+                for al in range(2):
+                    for u in range(2):
+                        nc.tensor.transpose(
+                            wt[:, u * 256 + al * P : u * 256 + (al + 1) * P],
+                            words[:, (2 * h + al) * 256 + u * P : (2 * h + al) * 256 + (u + 1) * P],
+                            ident[:],
+                        )
+                nc.scalar.copy(
+                    out=dst[:, 16 * h : 16 * (h + 1), i : i + KW, j : j + KW, :],
+                    in_=wt[:].rearrange("q (u c r v) -> q c r v u", u=2, c=16, r=KW, v=KW),
+                )
+            nc.vector.quantize_mx(out=wcod[p][:].bitcast(E4X4), scales=wsca[p][:], in_=wgrp[p][:])
+
+        def deinterleave(s):
+            tiles = []
+            for tl in range(GROUP):
+                t = gd_pool.tile([P, 4 * CO], BF16, name="gd")
+                nc.vector.tensor_copy(
+                    out=t[:].rearrange("q (p k) -> q p k", p=NPOS),
+                    in_=graw[s][:, tl * 4 * CO : (tl + 1) * 4 * CO].rearrange("q (k p) -> q p k", p=NPOS),
+                )
+                tiles.append(t)
+            gd[s] = tiles
+
+        def transposes(s):
+            banks = []
+            for tl in range(GROUP):
+                words = gd[s][tl][:].bitcast(F32)
+                for ph in range(2):
+                    t = psum_t.tile([P, NB], F32, name="gt")
+                    for pl in range(2):
+                        for u in range(2):
+                            nc.tensor.transpose(
+                                t[:, (pl * 2 + u) * P : (pl * 2 + u + 1) * P],
+                                words[:, (2 * ph + pl) * 256 + u * P : (2 * ph + pl) * 256 + (u + 1) * P],
+                                ident[:],
+                            )
+                    banks.append(t)
+            gt[s] = banks
+
+        def regroup_quantise(s):
+            res = []
+            for tl in range(GROUP):
+                grp = ggrp_pool.tile([P, 4 * NB], BF16, name="ggrp", align_bytes=64)
+                gw = grp[:].bitcast(F32)
+                for ph in range(2):
+                    nc.scalar.copy(
+                        out=gw[:, ph * NB : (ph + 1) * NB].rearrange("q (p b u) -> q p b u", p=2, u=2),
+                        in_=gt[s][tl * 2 + ph][:].rearrange("q (p u b) -> q p b u", p=2, u=2),
+                    )
+                cod = gq_pool.tile([P, NB], U32, name="gcod", align_bytes=64)
+                sca = gq_pool.tile([P, NB], U8, name="gsca", align_bytes=64)
+                nc.vector.quantize_mx(out=cod[:].bitcast(E5X4), scales=sca[:], in_=grp[:])
+                res.append((cod, sca))
+            gq[s] = res
+
+        def multiply_store(s):
+            acc = acc_pool.tile([P, GROUP * OUTC], F32, name="acc")
+            for tl in range(GROUP):
+                cod, sca = gq[s][tl]
+                bx = psum_m.tile([P, NB], F32, name="mx")
+                by = psum_m.tile([P, NB], F32, name="mx")
+                for p in range(NPOS):
+                    for half, bank in enumerate((bx, by)):
+                        nc.tensor.matmul_mx(
+                            out=bank[:],
+                            lhsT=cod[:, p * P : (p + 1) * P].bitcast(E5X4),
+                            lhsT_scale=sca[:, p * P : (p + 1) * P],
+                            rhs=wcod[p][:, half * NB : (half + 1) * NB].bitcast(E4X4),
+                            rhs_scale=wsca[p][:, half * NB : (half + 1) * NB],
+                            start=(p == 0),
+                            stop=(p == NPOS - 1),
+                        )
+                nc.scalar.copy(out=acc[:, tl * OUTC : tl * OUTC + NB], in_=bx[:])
+                nc.vector.tensor_copy(out=acc[:, tl * OUTC + NB : (tl + 1) * OUTC], in_=by[:, 0 : OUTC - NB])
+            nc.sync.dma_start(
+                out=o_view[:, GROUP * s : GROUP * (s + 1), :],
+                in_=acc[:].rearrange("q (n e) -> q n e", n=GROUP),
+            )
+
+        load_g(0)
+        for p in range(NPOS):
+            load_w(p)
+        for s in range(1, NG):
+            load_g(s)
+
+        deinterleave(0)
+        prep_w(0)
+        prep_w(1)
+        transposes(0)
+        regroup_quantise(0)
+        prep_w(2)
+        prep_w(3)
+        deinterleave(1)
+        transposes(1)
+        deinterleave(2)
+        for s in range(NG):
+            if s + 1 < NG:
+                regroup_quantise(s + 1)
+            multiply_store(s)
+            if s + 3 < NG:
+                deinterleave(s + 3)
+            if s + 2 < NG:
+                transposes(s + 2)

@@ -16,15 +16,13 @@ B, CI, CO, OH, OW, KW = 2048, 32, 512, 2, 2, 4
 IH, IW = 5, 5
 NPOS = OH * OW
 NT = B // P
-GROUP = 2
-NG = NT // GROUP
+NG = NT // 2
 OUTC = CI * IH * IW
+HC = OUTC // 2
 NB = 512
 
 FLOPS = 2 * NPOS * B * CO * CI * KW * KW
 BYTES = 2 * B * CO * NPOS + 2 * NPOS * CI * KW * KW * CO + 4 * B * OUTC
-
-PIN = False
 
 
 def tile_stdpconvinhibit_t_kernel(tc, in_spikes, weights, grad_out, out):
@@ -42,147 +40,203 @@ def tile_stdpconvinhibit_t_kernel(tc, in_spikes, weights, grad_out, out):
         acc_pool = ctx.enter_context(tc.tile_pool(name="acc", bufs=3))
         psum_t = ctx.enter_context(tc.psum_pool(name="psum_t", bufs=4))
         psum_m = ctx.enter_context(tc.psum_pool(name="psum_m", bufs=4))
-        if PIN:
-            ctx.enter_context(tc.manual_schedule())
+        ctx.enter_context(tc.manual_schedule())
 
         ident = const.tile([P, P], F32, name="ident")
         make_identity(nc, ident[:])
 
-        wraw = [const.tile([P, 4 * CO], BF16, name="wraw%d" % p) for p in range(NPOS)]
-        wgrp = [const.tile([P, 2 * NB * 4], BF16, name="wgrp%d" % p, align_bytes=64) for p in range(NPOS)]
-        wcod = [const.tile([P, 2 * NB], U32, name="wcod%d" % p, align_bytes=64) for p in range(NPOS)]
-        wsca = [const.tile([P, 2 * NB], U8, name="wsca%d" % p, align_bytes=64) for p in range(NPOS)]
-        for p in range(NPOS):
-            nc.vector.memset(wgrp[p][:].bitcast(I32), 0)
+        keys = [(p, h) for p in range(NPOS) for h in range(2)]
+        wraw = dict((k, const.tile([P, 2 * CO], BF16, name="wraw%d%d" % k)) for k in keys)
+        wgrp = dict((k, const.tile([P, NB * 4], BF16, name="wgrp%d%d" % k, align_bytes=64)) for k in keys)
+        wcod = dict((k, const.tile([P, NB], U32, name="wcod%d%d" % k, align_bytes=64)) for k in keys)
+        wsca = dict((k, const.tile([P, NB], U8, name="wsca%d%d" % k, align_bytes=64)) for k in keys)
+        for h in range(2):
+            for p in range(NPOS):
+                nc.vector.memset(wgrp[(p, h)][:].bitcast(I32), 0)
 
         graw = {}
         gd = {}
         gt = {}
         gq = {}
+        wt = {}
+        bank = {}
+        acc = {}
 
         def load_g(s):
-            t = graw_pool.tile([P, GROUP * 4 * CO], BF16, name="graw")
-            nc.sync.dma_start(
-                out=t[:].rearrange("q (n e) -> q n e", n=GROUP),
-                in_=g_view[:, GROUP * s : GROUP * (s + 1), :],
-            )
+            t = graw_pool.tile([P, 2 * 4 * CO], BF16, name="graw")
+            nc.sync.dma_start(out=t[:].rearrange("q (n e) -> q n e", n=2), in_=g_view[:, 2 * s : 2 * s + 2, :])
             graw[s] = t
 
-        def load_w(p):
+        def load_w(p, h):
             nc.sync.dma_start(
-                out=wraw[p][:].rearrange("q (n k) -> q n k", n=4),
-                in_=w_view[:, 4 * p : 4 * (p + 1), :],
+                out=wraw[(p, h)][:].rearrange("q (n k) -> q n k", n=2),
+                in_=w_view[:, 4 * p + 2 * h : 4 * p + 2 * h + 2, :],
             )
 
-        def prep_w(p):
+        def w_transpose(p, h, pool, tag):
+            words = wraw[(p, h)][:].bitcast(F32)
+            t = pool.tile([P, NB], F32, name=tag)
+            for al in range(2):
+                for u in range(2):
+                    nc.tensor.transpose(
+                        t[:, u * 256 + al * P : u * 256 + (al + 1) * P],
+                        words[:, al * 256 + u * P : al * 256 + (u + 1) * P],
+                        ident[:],
+                    )
+            wt[(p, h)] = t
+
+        def w_copy(p, h):
             i, j = p // OW, p % OW
-            words = wraw[p][:].bitcast(F32)
-            dst = wgrp[p][:].bitcast(F32)[:, 0 : OUTC * 2].rearrange(
-                "q (c y x u) -> q c y x u", c=CI, y=IH, x=IW, u=2
+            dst = wgrp[(p, h)][:].bitcast(F32)[:, 0 : HC * 2].rearrange(
+                "q (c y x u) -> q c y x u", c=16, y=IH, x=IW, u=2
             )
-            for h in range(2):
-                wt = psum_m.tile([P, NB], F32, name="mx")
-                for al in range(2):
+            nc.scalar.copy(
+                out=dst[:, :, i : i + KW, j : j + KW, :],
+                in_=wt[(p, h)][:].rearrange("q (u c r v) -> q c r v u", u=2, c=16, r=KW, v=KW),
+            )
+
+        def w_quantise(p, h):
+            nc.vector.quantize_mx(out=wcod[(p, h)][:].bitcast(E4X4), scales=wsca[(p, h)][:], in_=wgrp[(p, h)][:])
+
+        def deinterleave(n):
+            t = gd_pool.tile([P, 4 * CO], BF16, name="gd")
+            src = graw[n // 2][:, (n % 2) * 4 * CO : (n % 2 + 1) * 4 * CO]
+            nc.vector.tensor_copy(
+                out=t[:].rearrange("q (p k) -> q p k", p=NPOS),
+                in_=src.rearrange("q (k p) -> q p k", p=NPOS),
+            )
+            gd[n] = t
+
+        def transposes(n):
+            words = gd[n][:].bitcast(F32)
+            banks = []
+            for ph in range(2):
+                t = psum_t.tile([P, NB], F32, name="gt")
+                for pl in range(2):
                     for u in range(2):
                         nc.tensor.transpose(
-                            wt[:, u * 256 + al * P : u * 256 + (al + 1) * P],
-                            words[:, (2 * h + al) * 256 + u * P : (2 * h + al) * 256 + (u + 1) * P],
+                            t[:, (pl * 2 + u) * P : (pl * 2 + u + 1) * P],
+                            words[:, (2 * ph + pl) * 256 + u * P : (2 * ph + pl) * 256 + (u + 1) * P],
                             ident[:],
                         )
+                banks.append(t)
+            gt[n] = banks
+
+        def regroup(n):
+            grp = ggrp_pool.tile([P, 4 * NB], BF16, name="ggrp", align_bytes=64)
+            gw = grp[:].bitcast(F32)
+            for ph in range(2):
                 nc.scalar.copy(
-                    out=dst[:, 16 * h : 16 * (h + 1), i : i + KW, j : j + KW, :],
-                    in_=wt[:].rearrange("q (u c r v) -> q c r v u", u=2, c=16, r=KW, v=KW),
+                    out=gw[:, ph * NB : (ph + 1) * NB].rearrange("q (p b u) -> q p b u", p=2, u=2),
+                    in_=gt[n][ph][:].rearrange("q (p u b) -> q p b u", p=2, u=2),
                 )
-            nc.vector.quantize_mx(out=wcod[p][:].bitcast(E4X4), scales=wsca[p][:], in_=wgrp[p][:])
+            gt[n] = grp
 
-        def deinterleave(s):
-            tiles = []
-            for tl in range(GROUP):
-                t = gd_pool.tile([P, 4 * CO], BF16, name="gd")
-                nc.vector.tensor_copy(
-                    out=t[:].rearrange("q (p k) -> q p k", p=NPOS),
-                    in_=graw[s][:, tl * 4 * CO : (tl + 1) * 4 * CO].rearrange("q (k p) -> q p k", p=NPOS),
+        def quantise(n):
+            cod = gq_pool.tile([P, NB], U32, name="gcod", align_bytes=64)
+            sca = gq_pool.tile([P, NB], U8, name="gsca", align_bytes=64)
+            nc.vector.quantize_mx(out=cod[:].bitcast(E5X4), scales=sca[:], in_=gt[n][:])
+            gq[n] = (cod, sca)
+
+        def passes(n, h):
+            cod, sca = gq[n]
+            t = psum_m.tile([P, NB], F32, name="mx")
+            for p in range(NPOS):
+                nc.tensor.matmul_mx(
+                    out=t[:],
+                    lhsT=cod[:, p * P : (p + 1) * P].bitcast(E5X4),
+                    lhsT_scale=sca[:, p * P : (p + 1) * P],
+                    rhs=wcod[(p, h)][:].bitcast(E4X4),
+                    rhs_scale=wsca[(p, h)][:],
+                    start=(p == 0),
+                    stop=(p == NPOS - 1),
                 )
-                tiles.append(t)
-            gd[s] = tiles
+            bank[(n, h)] = t
 
-        def transposes(s):
-            banks = []
-            for tl in range(GROUP):
-                words = gd[s][tl][:].bitcast(F32)
-                for ph in range(2):
-                    t = psum_t.tile([P, NB], F32, name="gt")
-                    for pl in range(2):
-                        for u in range(2):
-                            nc.tensor.transpose(
-                                t[:, (pl * 2 + u) * P : (pl * 2 + u + 1) * P],
-                                words[:, (2 * ph + pl) * 256 + u * P : (2 * ph + pl) * 256 + (u + 1) * P],
-                                ident[:],
-                            )
-                    banks.append(t)
-            gt[s] = banks
+        def evacuate(n, h, on_vector=False):
+            if n % 2 == 0 and h == 0:
+                acc[n // 2] = acc_pool.tile([P, 2 * OUTC], F32, name="acc")
+            dst = acc[n // 2][:, (n % 2) * OUTC + h * HC : (n % 2) * OUTC + (h + 1) * HC]
+            if on_vector:
+                nc.vector.tensor_copy(out=dst, in_=bank[(n, h)][:, 0:HC])
+            else:
+                nc.scalar.copy(out=dst, in_=bank[(n, h)][:, 0:HC])
 
-        def regroup_quantise(s):
-            res = []
-            for tl in range(GROUP):
-                grp = ggrp_pool.tile([P, 4 * NB], BF16, name="ggrp", align_bytes=64)
-                gw = grp[:].bitcast(F32)
-                for ph in range(2):
-                    nc.scalar.copy(
-                        out=gw[:, ph * NB : (ph + 1) * NB].rearrange("q (p b u) -> q p b u", p=2, u=2),
-                        in_=gt[s][tl * 2 + ph][:].rearrange("q (p u b) -> q p b u", p=2, u=2),
-                    )
-                cod = gq_pool.tile([P, NB], U32, name="gcod", align_bytes=64)
-                sca = gq_pool.tile([P, NB], U8, name="gsca", align_bytes=64)
-                nc.vector.quantize_mx(out=cod[:].bitcast(E5X4), scales=sca[:], in_=grp[:])
-                res.append((cod, sca))
-            gq[s] = res
-
-        def multiply_store(s):
-            acc = acc_pool.tile([P, GROUP * OUTC], F32, name="acc")
-            for tl in range(GROUP):
-                cod, sca = gq[s][tl]
-                bx = psum_m.tile([P, NB], F32, name="mx")
-                by = psum_m.tile([P, NB], F32, name="mx")
-                for p in range(NPOS):
-                    for half, bank in enumerate((bx, by)):
-                        nc.tensor.matmul_mx(
-                            out=bank[:],
-                            lhsT=cod[:, p * P : (p + 1) * P].bitcast(E5X4),
-                            lhsT_scale=sca[:, p * P : (p + 1) * P],
-                            rhs=wcod[p][:, half * NB : (half + 1) * NB].bitcast(E4X4),
-                            rhs_scale=wsca[p][:, half * NB : (half + 1) * NB],
-                            start=(p == 0),
-                            stop=(p == NPOS - 1),
-                        )
-                nc.scalar.copy(out=acc[:, tl * OUTC : tl * OUTC + NB], in_=bx[:])
-                nc.vector.tensor_copy(out=acc[:, tl * OUTC + NB : (tl + 1) * OUTC], in_=by[:, 0 : OUTC - NB])
+        def store_pair(s):
             nc.sync.dma_start(
-                out=o_view[:, GROUP * s : GROUP * (s + 1), :],
-                in_=acc[:].rearrange("q (n e) -> q n e", n=GROUP),
+                out=o_view[:, 2 * s : 2 * s + 2, :], in_=acc[s][:].rearrange("q (n e) -> q n e", n=2)
             )
 
+        def store_one(n):
+            nc.sync.dma_start(out=o_view[:, n, :], in_=acc[n // 2][:, (n % 2) * OUTC : (n % 2 + 1) * OUTC])
+
+        for p in range(NPOS):
+            load_w(p, 0)
         load_g(0)
         for p in range(NPOS):
-            load_w(p)
+            load_w(p, 1)
         for s in range(1, NG):
             load_g(s)
 
+        for p in range(NPOS):
+            w_transpose(p, 0, psum_m, "mx")
+            w_copy(p, 0)
+            w_quantise(p, 0)
         deinterleave(0)
-        prep_w(0)
-        prep_w(1)
-        transposes(0)
-        regroup_quantise(0)
-        prep_w(2)
-        prep_w(3)
         deinterleave(1)
+        transposes(0)
+        regroup(0)
+        quantise(0)
+        for p in range(2):
+            w_transpose(p, 1, psum_m, "mx")
+            w_copy(p, 1)
+            w_quantise(p, 1)
         transposes(1)
+        w_transpose(2, 1, psum_t, "gt")
+        w_transpose(3, 1, psum_t, "gt")
+        passes(0, 0)
+        regroup(1)
+        quantise(1)
+        for p in range(2, NPOS):
+            w_copy(p, 1)
+            w_quantise(p, 1)
+        passes(1, 0)
+        evacuate(0, 0)
+        evacuate(1, 0)
         deinterleave(2)
-        for s in range(NG):
-            if s + 1 < NG:
-                regroup_quantise(s + 1)
-            multiply_store(s)
-            if s + 3 < NG:
-                deinterleave(s + 3)
-            if s + 2 < NG:
-                transposes(s + 2)
+        deinterleave(3)
+        passes(0, 1)
+        passes(1, 1)
+        evacuate(0, 1)
+        evacuate(1, 1)
+        store_pair(0)
+        transposes(2)
+        transposes(3)
+        deinterleave(4)
+        regroup(2)
+        quantise(2)
+        deinterleave(5)
+        regroup(3)
+        quantise(3)
+        transposes(4)
+        transposes(5)
+        for s in range(1, NG):
+            last = s == NG - 1
+            for n in (2 * s + 2, 2 * s + 3):
+                if n + 2 < NT:
+                    deinterleave(n + 2)
+                if n < NT:
+                    regroup(n)
+                    quantise(n)
+            for n in (2 * s, 2 * s + 1):
+                passes(n, 0)
+                passes(n, 1)
+                evacuate(n, 0)
+                evacuate(n, 1, on_vector=last)
+                if last:
+                    store_one(n)
+            if not last:
+                store_pair(s)
+            for n in (2 * s + 4, 2 * s + 5):
+                if n < NT:
+                    transposes(n)

@@ -46,13 +46,15 @@ def tile_stdpconvinhibit_t_kernel(tc, in_spikes, weights, grad_out, out):
         make_identity(nc, ident[:])
 
         keys = [(p, h) for p in range(NPOS) for h in range(2)]
+        keys_by_half = [(p, h) for h in range(2) for p in range(NPOS)]
         wraw = dict((k, const.tile([P, 2 * CO], BF16, name="wraw%d%d" % k)) for k in keys)
         wgrp = dict((k, const.tile([P, NB * 4], BF16, name="wgrp%d%d" % k, align_bytes=64)) for k in keys)
         wcod = dict((k, const.tile([P, NB], U32, name="wcod%d%d" % k, align_bytes=64)) for k in keys)
         wsca = dict((k, const.tile([P, NB], U8, name="wsca%d%d" % k, align_bytes=64)) for k in keys)
-        for h in range(2):
-            for p in range(NPOS):
-                nc.vector.memset(wgrp[(p, h)][:].bitcast(I32), 0)
+        for k in keys_by_half[:5]:
+            nc.vector.memset(wgrp[k][:].bitcast(I32), 0)
+        for k in keys_by_half[5:]:
+            nc.gpsimd.memset(wgrp[k][:].bitcast(F32), 0.0)
 
         graw = {}
         gd = {}
@@ -66,6 +68,11 @@ def tile_stdpconvinhibit_t_kernel(tc, in_spikes, weights, grad_out, out):
             t = graw_pool.tile([P, 2 * 4 * CO], BF16, name="graw")
             nc.sync.dma_start(out=t[:].rearrange("q (n e) -> q n e", n=2), in_=g_view[:, 2 * s : 2 * s + 2, :])
             graw[s] = t
+
+        def load_g_tile(n):
+            if n == 0:
+                graw[0] = graw_pool.tile([P, 2 * 4 * CO], BF16, name="graw")
+            nc.sync.dma_start(out=graw[0][:, n * 4 * CO : (n + 1) * 4 * CO], in_=g_view[:, n, :])
 
         def load_w(p, h):
             nc.sync.dma_start(
@@ -167,45 +174,69 @@ def tile_stdpconvinhibit_t_kernel(tc, in_spikes, weights, grad_out, out):
                 out=o_view[:, 2 * s : 2 * s + 2, :], in_=acc[s][:].rearrange("q (n e) -> q n e", n=2)
             )
 
+        def store_half(n, h):
+            lo = (n % 2) * OUTC + h * HC
+            nc.sync.dma_start(out=o_view[:, n, h * HC : (h + 1) * HC], in_=acc[n // 2][:, lo : lo + HC])
+
         def store_one(n):
             nc.sync.dma_start(out=o_view[:, n, :], in_=acc[n // 2][:, (n % 2) * OUTC : (n % 2 + 1) * OUTC])
 
-        for p in range(NPOS):
-            load_w(p, 0)
-        load_g(0)
+        def w_prepare(p, h):
+            w_transpose(p, h, psum_m, "mx")
+            w_copy(p, h)
+
+        def multiply(n, last=False):
+            passes(n, 0)
+            passes(n, 1)
+            evacuate(n, 0)
+            if last:
+                store_half(n, 0)
+            evacuate(n, 1, on_vector=last)
+            if last:
+                store_half(n, 1)
+
+        load_w(0, 0)
+        load_w(1, 0)
+        load_g_tile(0)
+        load_w(2, 0)
+        load_w(3, 0)
+        load_g_tile(1)
         for p in range(NPOS):
             load_w(p, 1)
         for s in range(1, NG):
             load_g(s)
 
-        for p in range(NPOS):
-            w_transpose(p, 0, psum_m, "mx")
-            w_copy(p, 0)
-            w_quantise(p, 0)
+        w_prepare(0, 0)
+        w_prepare(1, 0)
         deinterleave(0)
-        deinterleave(1)
+        w_quantise(0, 0)
+        w_quantise(1, 0)
         transposes(0)
+        w_prepare(2, 0)
+        w_prepare(3, 0)
         regroup(0)
+        deinterleave(1)
         quantise(0)
-        for p in range(2):
-            w_transpose(p, 1, psum_m, "mx")
-            w_copy(p, 1)
-            w_quantise(p, 1)
+        w_quantise(2, 0)
+        w_quantise(3, 0)
         transposes(1)
-        w_transpose(2, 1, psum_t, "gt")
-        w_transpose(3, 1, psum_t, "gt")
-        passes(0, 0)
+        w_prepare(0, 1)
+        w_prepare(1, 1)
         regroup(1)
+        w_quantise(0, 1)
         quantise(1)
-        for p in range(2, NPOS):
-            w_copy(p, 1)
-            w_quantise(p, 1)
+        w_prepare(2, 1)
+        w_prepare(3, 1)
+        passes(0, 0)
+        w_quantise(1, 1)
+        w_quantise(2, 1)
+        w_quantise(3, 1)
         passes(1, 0)
         evacuate(0, 0)
         evacuate(1, 0)
+        passes(0, 1)
         deinterleave(2)
         deinterleave(3)
-        passes(0, 1)
         passes(1, 1)
         evacuate(0, 1)
         evacuate(1, 1)
@@ -218,25 +249,17 @@ def tile_stdpconvinhibit_t_kernel(tc, in_spikes, weights, grad_out, out):
         deinterleave(5)
         regroup(3)
         quantise(3)
-        transposes(4)
-        transposes(5)
-        for s in range(1, NG):
-            last = s == NG - 1
-            for n in (2 * s + 2, 2 * s + 3):
+        multiply(2)
+        for a in range(4, NT, 2):
+            transposes(a)
+            transposes(a + 1)
+            for n in (a, a + 1):
                 if n + 2 < NT:
                     deinterleave(n + 2)
-                if n < NT:
-                    regroup(n)
-                    quantise(n)
-            for n in (2 * s, 2 * s + 1):
-                passes(n, 0)
-                passes(n, 1)
-                evacuate(n, 0)
-                evacuate(n, 1, on_vector=last)
-                if last:
-                    store_one(n)
-            if not last:
-                store_pair(s)
-            for n in (2 * s + 4, 2 * s + 5):
-                if n < NT:
-                    transposes(n)
+                regroup(n)
+                quantise(n)
+            multiply(a - 1)
+            store_pair((a - 1) // 2)
+            multiply(a)
+        store_one(NT - 2)
+        multiply(NT - 1, last=True)

@@ -23,6 +23,8 @@ NB = 512
 
 FLOPS = 2 * NPOS * B * CO * CI * KW * KW
 BYTES = 2 * B * CO * NPOS + 2 * NPOS * CI * KW * KW * CO + 4 * B * OUTC
+PAD = 48
+SLOT = 256
 
 
 def tile_stdpconvinhibit_t_kernel(tc, in_spikes, weights, grad_out, out):
@@ -49,8 +51,8 @@ def tile_stdpconvinhibit_t_kernel(tc, in_spikes, weights, grad_out, out):
         keys_by_half = [(p, h) for h in range(2) for p in range(NPOS)]
         wraw = dict((k, const.tile([P, 2 * CO], BF16, name="wraw%d%d" % k)) for k in keys)
         wgrp = dict((k, const.tile([P, NB * 4], BF16, name="wgrp%d%d" % k, align_bytes=64)) for k in keys)
-        wcod = dict((k, const.tile([P, NB], U32, name="wcod%d%d" % k, align_bytes=64)) for k in keys)
-        wsca = dict((k, const.tile([P, NB], U8, name="wsca%d%d" % k, align_bytes=64)) for k in keys)
+        wcod = dict((k, const.tile([P, NB], U32, name="wcod%d%d" % k, align_bytes=256)) for k in keys)
+        wsca = dict((k, const.tile([P, NB], U8, name="wsca%d%d" % k, align_bytes=256)) for k in keys)
         for k in keys_by_half[:5]:
             nc.vector.memset(wgrp[k][:].bitcast(I32), 0)
         for k in keys_by_half[5:]:
@@ -140,9 +142,14 @@ def tile_stdpconvinhibit_t_kernel(tc, in_spikes, weights, grad_out, out):
             gt[n] = grp
 
         def quantise(n):
-            cod = gq_pool.tile([P, NB], U32, name="gcod", align_bytes=64)
-            sca = gq_pool.tile([P, NB], U8, name="gsca", align_bytes=64)
-            nc.vector.quantize_mx(out=cod[:].bitcast(E5X4), scales=sca[:], in_=gt[n][:])
+            cod = gq_pool.tile([P, PAD + NB], U32, name="gcod", align_bytes=256)
+            sca = gq_pool.tile([P, NPOS * SLOT], U8, name="gsca", align_bytes=256)
+            for p in range(NPOS):
+                nc.vector.quantize_mx(
+                    out=cod[:, PAD + p * P : PAD + (p + 1) * P].bitcast(E5X4),
+                    scales=sca[:, p * SLOT : p * SLOT + P],
+                    in_=gt[n][:, p * NB : (p + 1) * NB],
+                )
             gq[n] = (cod, sca)
 
         def passes(n, h):
@@ -151,8 +158,8 @@ def tile_stdpconvinhibit_t_kernel(tc, in_spikes, weights, grad_out, out):
             for p in range(NPOS):
                 nc.tensor.matmul_mx(
                     out=t[:],
-                    lhsT=cod[:, p * P : (p + 1) * P].bitcast(E5X4),
-                    lhsT_scale=sca[:, p * P : (p + 1) * P],
+                    lhsT=cod[:, PAD + p * P : PAD + (p + 1) * P].bitcast(E5X4),
+                    lhsT_scale=sca[:, p * SLOT : p * SLOT + P],
                     rhs=wcod[(p, h)][:].bitcast(E4X4),
                     rhs_scale=wsca[(p, h)][:],
                     start=(p == 0),
@@ -211,9 +218,9 @@ def tile_stdpconvinhibit_t_kernel(tc, in_spikes, weights, grad_out, out):
         deinterleave(0)
         w_quantise(0, 0)
         w_quantise(1, 0)
-        transposes(0)
         w_prepare(2, 0)
         w_prepare(3, 0)
+        transposes(0)
         regroup(0)
         deinterleave(1)
         quantise(0)

@@ -25,6 +25,8 @@ FLOPS = 2 * NPOS * B * CO * CI * KW * KW
 BYTES = 2 * B * CO * NPOS + 2 * NPOS * CI * KW * KW * CO + 4 * B * OUTC
 PAD = 48
 SLOT = 256
+WQ_WIDTHS = (256, 128, 32)
+WQ_COLS = 416
 
 
 def tile_stdpconvinhibit_t_kernel(tc, in_spikes, weights, grad_out, out):
@@ -53,10 +55,13 @@ def tile_stdpconvinhibit_t_kernel(tc, in_spikes, weights, grad_out, out):
         wgrp = dict((k, const.tile([P, NB * 4], BF16, name="wgrp%d%d" % k, align_bytes=64)) for k in keys)
         wcod = dict((k, const.tile([P, NB], U32, name="wcod%d%d" % k, align_bytes=256)) for k in keys)
         wsca = dict((k, const.tile([P, NB], U8, name="wsca%d%d" % k, align_bytes=256)) for k in keys)
-        for k in keys_by_half[:5]:
-            nc.vector.memset(wgrp[k][:].bitcast(I32), 0)
-        for k in keys_by_half[5:]:
-            nc.gpsimd.memset(wgrp[k][:].bitcast(F32), 0.0)
+        for k in keys_by_half[:4]:
+            nc.vector.memset(wgrp[k][:, 0 : 4 * WQ_COLS].bitcast(I32), 0)
+        for k in keys_by_half[4:]:
+            nc.gpsimd.memset(wgrp[k][:, 0 : 4 * WQ_COLS].bitcast(F32), 0.0)
+        for k in keys_by_half:
+            nc.vector.memset(wcod[k][:, WQ_COLS:NB].bitcast(I32), 0)
+            nc.vector.memset(wsca[k][:, WQ_COLS:NB].bitcast(I32), 0)
 
         graw = {}
         gd = {}
@@ -105,15 +110,22 @@ def tile_stdpconvinhibit_t_kernel(tc, in_spikes, weights, grad_out, out):
             )
 
         def w_quantise(p, h):
-            nc.vector.quantize_mx(out=wcod[(p, h)][:].bitcast(E4X4), scales=wsca[(p, h)][:], in_=wgrp[(p, h)][:])
+            lo = 0
+            for width in WQ_WIDTHS:
+                nc.vector.quantize_mx(
+                    out=wcod[(p, h)][:, lo : lo + width].bitcast(E4X4),
+                    scales=wsca[(p, h)][:, lo : lo + width],
+                    in_=wgrp[(p, h)][:, 4 * lo : 4 * (lo + width)],
+                )
+                lo += width
 
         def deinterleave(n):
             t = gd_pool.tile([P, 4 * CO], BF16, name="gd")
             src = graw[n // 2][:, (n % 2) * 4 * CO : (n % 2 + 1) * 4 * CO]
-            nc.vector.tensor_copy(
-                out=t[:].rearrange("q (p k) -> q p k", p=NPOS),
-                in_=src.rearrange("q (k p) -> q p k", p=NPOS),
-            )
+            dst = t[:].rearrange("q (p k) -> q p k", p=NPOS)
+            srcv = src.rearrange("q (k p) -> q p k", p=NPOS)
+            for ph in range(2):
+                nc.vector.tensor_copy(out=dst[:, 2 * ph : 2 * ph + 2, :], in_=srcv[:, 2 * ph : 2 * ph + 2, :])
             gd[n] = t
 
         def transposes(n):
@@ -202,9 +214,9 @@ def tile_stdpconvinhibit_t_kernel(tc, in_spikes, weights, grad_out, out):
             if last:
                 store_half(n, 1)
 
+        load_g_tile(0)
         load_w(0, 0)
         load_w(1, 0)
-        load_g_tile(0)
         load_w(2, 0)
         load_w(3, 0)
         load_g_tile(1)
@@ -213,14 +225,14 @@ def tile_stdpconvinhibit_t_kernel(tc, in_spikes, weights, grad_out, out):
         for s in range(1, NG):
             load_g(s)
 
+        deinterleave(0)
         w_prepare(0, 0)
         w_prepare(1, 0)
-        deinterleave(0)
         w_quantise(0, 0)
         w_quantise(1, 0)
+        transposes(0)
         w_prepare(2, 0)
         w_prepare(3, 0)
-        transposes(0)
         regroup(0)
         deinterleave(1)
         quantise(0)

@@ -25,8 +25,6 @@ FLOPS = 2 * NPOS * B * CO * CI * KW * KW
 BYTES = 2 * B * CO * NPOS + 2 * NPOS * CI * KW * KW * CO + 4 * B * OUTC
 PAD = 48
 SLOT = 256
-WQ_WIDTHS = (256, 128, 32)
-WQ_COLS = 416
 
 
 def tile_stdpconvinhibit_t_kernel(tc, in_spikes, weights, grad_out, out):
@@ -55,13 +53,10 @@ def tile_stdpconvinhibit_t_kernel(tc, in_spikes, weights, grad_out, out):
         wgrp = dict((k, const.tile([P, NB * 4], BF16, name="wgrp%d%d" % k, align_bytes=64)) for k in keys)
         wcod = dict((k, const.tile([P, NB], U32, name="wcod%d%d" % k, align_bytes=256)) for k in keys)
         wsca = dict((k, const.tile([P, NB], U8, name="wsca%d%d" % k, align_bytes=256)) for k in keys)
-        for k in keys_by_half[:4]:
-            nc.vector.memset(wgrp[k][:, 0 : 4 * WQ_COLS].bitcast(I32), 0)
-        for k in keys_by_half[4:]:
-            nc.gpsimd.memset(wgrp[k][:, 0 : 4 * WQ_COLS].bitcast(F32), 0.0)
-        for k in keys_by_half:
-            nc.vector.memset(wcod[k][:, WQ_COLS:NB].bitcast(I32), 0)
-            nc.vector.memset(wsca[k][:, WQ_COLS:NB].bitcast(I32), 0)
+        for k in keys_by_half[:5]:
+            nc.vector.memset(wgrp[k][:].bitcast(I32), 0)
+        for k in keys_by_half[5:]:
+            nc.gpsimd.memset(wgrp[k][:].bitcast(F32), 0.0)
 
         graw = {}
         gd = {}
@@ -110,22 +105,15 @@ def tile_stdpconvinhibit_t_kernel(tc, in_spikes, weights, grad_out, out):
             )
 
         def w_quantise(p, h):
-            lo = 0
-            for width in WQ_WIDTHS:
-                nc.vector.quantize_mx(
-                    out=wcod[(p, h)][:, lo : lo + width].bitcast(E4X4),
-                    scales=wsca[(p, h)][:, lo : lo + width],
-                    in_=wgrp[(p, h)][:, 4 * lo : 4 * (lo + width)],
-                )
-                lo += width
+            nc.vector.quantize_mx(out=wcod[(p, h)][:].bitcast(E4X4), scales=wsca[(p, h)][:], in_=wgrp[(p, h)][:])
 
         def deinterleave(n):
             t = gd_pool.tile([P, 4 * CO], BF16, name="gd")
             src = graw[n // 2][:, (n % 2) * 4 * CO : (n % 2 + 1) * 4 * CO]
-            dst = t[:].rearrange("q (p k) -> q p k", p=NPOS)
-            srcv = src.rearrange("q (k p) -> q p k", p=NPOS)
-            for ph in range(2):
-                nc.vector.tensor_copy(out=dst[:, 2 * ph : 2 * ph + 2, :], in_=srcv[:, 2 * ph : 2 * ph + 2, :])
+            nc.vector.tensor_copy(
+                out=t[:].rearrange("q (p c i) -> q c p i", p=NPOS, i=4),
+                in_=src.rearrange("q (c i p) -> q c p i", i=4, p=NPOS),
+            )
             gd[n] = t
 
         def transposes(n):
@@ -214,9 +202,9 @@ def tile_stdpconvinhibit_t_kernel(tc, in_spikes, weights, grad_out, out):
             if last:
                 store_half(n, 1)
 
-        load_g_tile(0)
         load_w(0, 0)
         load_w(1, 0)
+        load_g_tile(0)
         load_w(2, 0)
         load_w(3, 0)
         load_g_tile(1)
@@ -225,14 +213,14 @@ def tile_stdpconvinhibit_t_kernel(tc, in_spikes, weights, grad_out, out):
         for s in range(1, NG):
             load_g(s)
 
-        deinterleave(0)
         w_prepare(0, 0)
         w_prepare(1, 0)
+        deinterleave(0)
         w_quantise(0, 0)
         w_quantise(1, 0)
-        transposes(0)
         w_prepare(2, 0)
         w_prepare(3, 0)
+        transposes(0)
         regroup(0)
         deinterleave(1)
         quantise(0)

@@ -203,11 +203,11 @@ def tile_stdpconvinhibit_t_kernel(tc, in_spikes, weights, grad_out, out):
                 store_half(n, 1)
 
         load_w(0, 0)
-        load_w(1, 0)
         load_g_tile(0)
+        load_w(1, 0)
         load_w(2, 0)
-        load_w(3, 0)
         load_g_tile(1)
+        load_w(3, 0)
         for p in range(NPOS):
             load_w(p, 1)
         for s in range(1, NG):
@@ -215,58 +215,55 @@ def tile_stdpconvinhibit_t_kernel(tc, in_spikes, weights, grad_out, out):
 
         w_prepare(0, 0)
         w_prepare(1, 0)
-        deinterleave(0)
-        w_quantise(0, 0)
-        w_quantise(1, 0)
         w_prepare(2, 0)
-        w_prepare(3, 0)
+        deinterleave(0)
         transposes(0)
         regroup(0)
+        w_prepare(3, 0)
+        w_quantise(0, 0)
+        w_quantise(1, 0)
         deinterleave(1)
         quantise(0)
         w_quantise(2, 0)
         w_quantise(3, 0)
         transposes(1)
-        w_prepare(0, 1)
-        w_prepare(1, 1)
         regroup(1)
-        w_quantise(0, 1)
+        for p in range(NPOS):
+            w_prepare(p, 1)
         quantise(1)
-        w_prepare(2, 1)
-        w_prepare(3, 1)
-        passes(0, 0)
-        w_quantise(1, 1)
-        w_quantise(2, 1)
-        w_quantise(3, 1)
-        passes(1, 0)
-        evacuate(0, 0)
-        evacuate(1, 0)
-        passes(0, 1)
+        for p in range(NPOS):
+            w_quantise(p, 1)
         deinterleave(2)
         deinterleave(3)
+        passes(0, 0)
+        passes(1, 0)
+        passes(0, 1)
         passes(1, 1)
+        evacuate(0, 0)
+        evacuate(1, 0)
         evacuate(0, 1)
         evacuate(1, 1)
         store_pair(0)
         transposes(2)
         transposes(3)
-        deinterleave(4)
         regroup(2)
-        quantise(2)
-        deinterleave(5)
         regroup(3)
-        quantise(3)
+        quantise(2)
+        deinterleave(4)
         multiply(2)
-        for a in range(4, NT, 2):
-            transposes(a)
-            transposes(a + 1)
-            for n in (a, a + 1):
-                if n + 2 < NT:
-                    deinterleave(n + 2)
-                regroup(n)
-                quantise(n)
-            multiply(a - 1)
-            store_pair((a - 1) // 2)
-            multiply(a)
+        for n in range(3, NT - 2, 2):
+            deinterleave(n + 2)
+            transposes(n + 1)
+            transposes(n + 2)
+            quantise(n)
+            regroup(n + 1)
+            if n + 3 < NT:
+                deinterleave(n + 3)
+            quantise(n + 1)
+            regroup(n + 2)
+            multiply(n)
+            store_pair(n // 2)
+            multiply(n + 1)
+        quantise(NT - 1)
         store_one(NT - 2)
         multiply(NT - 1, last=True)

@@ -23,6 +23,7 @@ NB = 512
 
 FLOPS = 2 * NPOS * B * CO * CI * KW * KW
 BYTES = 2 * B * CO * NPOS + 2 * NPOS * CI * KW * KW * CO + 4 * B * OUTC
+JUNK = NB - HC
 PAD = 48
 SLOT = 256
 
@@ -50,13 +51,34 @@ def tile_stdpconvinhibit_t_kernel(tc, in_spikes, weights, grad_out, out):
         keys = [(p, h) for p in range(NPOS) for h in range(2)]
         keys_by_half = [(p, h) for h in range(2) for p in range(NPOS)]
         wraw = dict((k, const.tile([P, 2 * CO], BF16, name="wraw%d%d" % k)) for k in keys)
-        wgrp = dict((k, const.tile([P, NB * 4], BF16, name="wgrp%d%d" % k, align_bytes=64)) for k in keys)
+        wall = const.tile([P, (JUNK + 2 * NPOS * HC) * 4], BF16, name="wall", align_bytes=64)
+        wwords = wall[:].bitcast(F32)
+        wints = wall[:].bitcast(I32)
+        rank = dict((k, r) for r, k in enumerate(keys_by_half))
+        ROW = IW * 16 * 2
+        CELL = 16 * 2
         wcod = dict((k, const.tile([P, NB], U32, name="wcod%d%d" % k, align_bytes=256)) for k in keys)
         wsca = dict((k, const.tile([P, NB], U8, name="wsca%d%d" % k, align_bytes=256)) for k in keys)
-        for k in keys_by_half[:5]:
-            nc.vector.memset(wgrp[k][:].bitcast(I32), 0)
-        for k in keys_by_half[5:]:
-            nc.gpsimd.memset(wgrp[k][:].bitcast(F32), 0.0)
+        def w_base(p, h):
+            return (JUNK + rank[(p, h)] * HC) * 2
+
+        def w_zero(p, h):
+            i, j = p // OW, p % OW
+            lo = w_base(p, h)
+            y0 = (IH - 1) * (1 - i)
+            x0 = (IW - 1) * (1 - j)
+            if h == 0:
+                nc.vector.memset(wints[:, lo + y0 * ROW : lo + (y0 + 1) * ROW], 0)
+                rows = wints[:, lo + i * ROW : lo + (i + KW) * ROW].rearrange("q (y w) -> q y w", y=KW)
+                nc.vector.memset(rows[:, :, x0 * CELL : (x0 + 1) * CELL], 0)
+            else:
+                nc.gpsimd.memset(wwords[:, lo + y0 * ROW : lo + (y0 + 1) * ROW], 0.0)
+                rows = wwords[:, lo + i * ROW : lo + (i + KW) * ROW].rearrange("q (y w) -> q y w", y=KW)
+                nc.gpsimd.memset(rows[:, :, x0 * CELL : (x0 + 1) * CELL], 0.0)
+
+        nc.vector.memset(wints[:, 0 : JUNK * 2], 0)
+        for k in keys_by_half:
+            w_zero(k[0], k[1])
 
         graw = {}
         gd = {}
@@ -96,16 +118,20 @@ def tile_stdpconvinhibit_t_kernel(tc, in_spikes, weights, grad_out, out):
 
         def w_copy(p, h):
             i, j = p // OW, p % OW
-            dst = wgrp[(p, h)][:].bitcast(F32)[:, 0 : HC * 2].rearrange(
-                "q (c y x u) -> q c y x u", c=16, y=IH, x=IW, u=2
+            lo = w_base(p, h)
+            dst = wwords[:, lo + i * ROW : lo + (i + KW) * ROW].rearrange(
+                "q (y x c u) -> q y x c u", y=KW, x=IW, c=16, u=2
             )
             nc.scalar.copy(
-                out=dst[:, :, i : i + KW, j : j + KW, :],
-                in_=wt[(p, h)][:].rearrange("q (u c r v) -> q c r v u", u=2, c=16, r=KW, v=KW),
+                out=dst[:, :, j : j + KW, :, :],
+                in_=wt[(p, h)][:].rearrange("q (u c r v) -> q r v c u", u=2, c=16, r=KW, v=KW),
             )
 
         def w_quantise(p, h):
-            nc.vector.quantize_mx(out=wcod[(p, h)][:].bitcast(E4X4), scales=wsca[(p, h)][:], in_=wgrp[(p, h)][:])
+            lo = rank[(p, h)] * HC * 4
+            nc.vector.quantize_mx(
+                out=wcod[(p, h)][:].bitcast(E4X4), scales=wsca[(p, h)][:], in_=wall[:, lo : lo + NB * 4]
+            )
 
         def deinterleave(n):
             t = gd_pool.tile([P, 4 * CO], BF16, name="gd")
@@ -170,11 +196,14 @@ def tile_stdpconvinhibit_t_kernel(tc, in_spikes, weights, grad_out, out):
         def evacuate(n, h, on_vector=False):
             if n % 2 == 0 and h == 0:
                 acc[n // 2] = acc_pool.tile([P, 2 * OUTC], F32, name="acc")
-            dst = acc[n // 2][:, (n % 2) * OUTC + h * HC : (n % 2) * OUTC + (h + 1) * HC]
+            dst = acc[n // 2][:, (n % 2) * OUTC + h * HC : (n % 2) * OUTC + (h + 1) * HC].rearrange(
+                "q (c s) -> q c s", c=16
+            )
+            src = bank[(n, h)][:, JUNK:NB].rearrange("q (s c) -> q c s", c=16)
             if on_vector:
-                nc.vector.tensor_copy(out=dst, in_=bank[(n, h)][:, 0:HC])
+                nc.vector.tensor_copy(out=dst, in_=src)
             else:
-                nc.scalar.copy(out=dst, in_=bank[(n, h)][:, 0:HC])
+                nc.scalar.copy(out=dst, in_=src)
 
         def store_pair(s):
             nc.sync.dma_start(

@@ -217,8 +217,11 @@ def tile_stdpconvinhibit_t_kernel(tc, in_spikes, weights, grad_out, out):
         def store_one(n):
             nc.sync.dma_start(out=o_view[:, n, :], in_=acc[n // 2][:, (n % 2) * OUTC : (n % 2 + 1) * OUTC])
 
-        def w_prepare(p, h):
-            w_transpose(p, h, psum_m, "mx")
+        def w_prepare(p, h, in_transpose_banks=False):
+            if in_transpose_banks:
+                w_transpose(p, h, psum_t, "gt")
+            else:
+                w_transpose(p, h, psum_m, "mx")
             w_copy(p, h)
 
         def multiply(n, last=False):
@@ -250,15 +253,15 @@ def tile_stdpconvinhibit_t_kernel(tc, in_spikes, weights, grad_out, out):
         regroup(0)
         w_prepare(3, 0)
         w_quantise(0, 0)
-        w_quantise(1, 0)
         deinterleave(1)
-        quantise(0)
+        w_quantise(1, 0)
         w_quantise(2, 0)
+        quantise(0)
         w_quantise(3, 0)
         transposes(1)
         regroup(1)
         for p in range(NPOS):
-            w_prepare(p, 1)
+            w_prepare(p, 1, in_transpose_banks=(p < 2))
         quantise(1)
         for p in range(NPOS):
             w_quantise(p, 1)

@@ -24,7 +24,7 @@ NB = 512
 FLOPS = 2 * NPOS * B * CO * CI * KW * KW
 BYTES = 2 * B * CO * NPOS + 2 * NPOS * CI * KW * KW * CO + 4 * B * OUTC
 JUNK = NB - HC
-PAD = 48
+PAD = 32
 SLOT = 256
 
 

@@ -16,31 +16,37 @@ B, CI, CO, OH, OW, KW = 2048, 32, 512, 2, 2, 4
 IH, IW = 5, 5
 NPOS = OH * OW
 NT = B // P
-NG = NT // 2
 OUTC = CI * IH * IW
 HC = OUTC // 2
 NB = 512
 
 FLOPS = 2 * NPOS * B * CO * CI * KW * KW
 BYTES = 2 * B * CO * NPOS + 2 * NPOS * CI * KW * KW * CO + 4 * B * OUTC
-JUNK = NB - HC
 PAD = 32
-SLOT = 256
+VT_TILES = [5, 7, 9, 11, 13, 15]
+T_TILES = [n for n in range(NT) if n not in VT_TILES]
+NTT = len(T_TILES)
+FIRST = 48
+PIX = 16
+QUANT = {0: ((0, 256), (256, 128)), 1: ((128, 256), (384, 64))}
+FILL = {0: ((384, 512),), 1: ((0, 128), (448, 512))}
 
 
 def tile_stdpconvinhibit_t_kernel(tc, in_spikes, weights, grad_out, out):
     nc = tc.nc
-    g_view = grad_out.rearrange("(q n) k i j -> q n (k i j)", n=NT)
-    o_view = out.rearrange("(q n) c h w -> q n (c h w)", n=NT)
+    split = P * NTT
+    gt_view = grad_out[0:split].rearrange("(q n) k i j -> q n (k i j)", n=NTT)
+    ot_view = out[0:split].rearrange("(q n) c h w -> q n (c h w)", n=NTT)
+    gv_view = grad_out[split:B].rearrange("(g b) k i j -> b g (k i j)", b=16)
+    ov_view = out[split:B].rearrange("(n q) c h w -> n q (c h w)", q=P)
     w_view = weights.rearrange("i j c u v k -> (i j c u v) k").rearrange("(n q) k -> q n k", q=P)
 
     with ExitStack() as ctx:
         const = ctx.enter_context(tc.tile_pool(name="const", bufs=1))
-        graw_pool = ctx.enter_context(tc.tile_pool(name="graw", bufs=NG))
-        gd_pool = ctx.enter_context(tc.tile_pool(name="gd", bufs=4))
+        gd_pool = ctx.enter_context(tc.tile_pool(name="gd", bufs=6))
         ggrp_pool = ctx.enter_context(tc.tile_pool(name="ggrp", bufs=4))
         gq_pool = ctx.enter_context(tc.tile_pool(name="gq", bufs=6))
-        acc_pool = ctx.enter_context(tc.tile_pool(name="acc", bufs=3))
+        acc_pool = ctx.enter_context(tc.tile_pool(name="acc", bufs=6))
         psum_t = ctx.enter_context(tc.psum_pool(name="psum_t", bufs=4))
         psum_m = ctx.enter_context(tc.psum_pool(name="psum_m", bufs=4))
         ctx.enter_context(tc.manual_schedule())
@@ -49,36 +55,44 @@ def tile_stdpconvinhibit_t_kernel(tc, in_spikes, weights, grad_out, out):
         make_identity(nc, ident[:])
 
         keys = [(p, h) for p in range(NPOS) for h in range(2)]
-        keys_by_half = [(p, h) for h in range(2) for p in range(NPOS)]
         wraw = dict((k, const.tile([P, 2 * CO], BF16, name="wraw%d%d" % k)) for k in keys)
-        wall = const.tile([P, (JUNK + 2 * NPOS * HC) * 4], BF16, name="wall", align_bytes=64)
-        wwords = wall[:].bitcast(F32)
-        wints = wall[:].bitcast(I32)
-        rank = dict((k, r) for r, k in enumerate(keys_by_half))
-        ROW = IW * 16 * 2
-        CELL = 16 * 2
         wcod = dict((k, const.tile([P, NB], U32, name="wcod%d%d" % k, align_bytes=256)) for k in keys)
         wsca = dict((k, const.tile([P, NB], U8, name="wsca%d%d" % k, align_bytes=256)) for k in keys)
-        def w_base(p, h):
-            return (JUNK + rank[(p, h)] * HC) * 2
+        wpad = dict(
+            (k, const.tile([P, 4 * sum(w for s, w in QUANT[k[0] // OW])], BF16, name="wpad%d%d" % k, align_bytes=64))
+            for k in keys
+        )
+
+        def w_rows(p, h):
+            i = p // OW
+            lo = (FIRST + i * IW * PIX - QUANT[i][0][0]) * 2
+            words = wpad[(p, h)][:].bitcast(F32)[:, lo : lo + KW * IW * PIX * 2]
+            return words.rearrange("q (y x e) -> q y x e", y=KW, x=IW)
 
         def w_zero(p, h):
             i, j = p // OW, p % OW
-            lo = w_base(p, h)
-            y0 = (IH - 1) * (1 - i)
+            ints = wpad[(p, h)][:].bitcast(I32)
+            lo = (FIRST + i * IW * PIX - QUANT[i][0][0]) * 2
+            hi = lo + KW * IW * PIX * 2
+            end = 2 * sum(w for s, w in QUANT[i])
+            if lo > 0:
+                nc.vector.memset(ints[:, 0:lo], 0)
+            if hi < end:
+                nc.vector.memset(ints[:, hi:end], 0)
+            rows = ints[:, lo:hi].rearrange("q (y x e) -> q y x e", y=KW, x=IW)
             x0 = (IW - 1) * (1 - j)
-            if h == 0:
-                nc.vector.memset(wints[:, lo + y0 * ROW : lo + (y0 + 1) * ROW], 0)
-                rows = wints[:, lo + i * ROW : lo + (i + KW) * ROW].rearrange("q (y w) -> q y w", y=KW)
-                nc.vector.memset(rows[:, :, x0 * CELL : (x0 + 1) * CELL], 0)
-            else:
-                nc.gpsimd.memset(wwords[:, lo + y0 * ROW : lo + (y0 + 1) * ROW], 0.0)
-                rows = wwords[:, lo + i * ROW : lo + (i + KW) * ROW].rearrange("q (y w) -> q y w", y=KW)
-                nc.gpsimd.memset(rows[:, :, x0 * CELL : (x0 + 1) * CELL], 0.0)
+            nc.vector.memset(rows[:, :, x0, :], 0)
 
-        nc.vector.memset(wints[:, 0 : JUNK * 2], 0)
-        for k in keys_by_half:
-            w_zero(k[0], k[1])
+        def w_fill(p, h):
+            scales = wsca[(p, h)][:].bitcast(I32)
+            for lo, hi in FILL[p // OW]:
+                nc.gpsimd.memset(wcod[(p, h)][:, lo:hi], 0)
+                nc.gpsimd.memset(scales[:, lo // 4 : hi // 4], 0)
+
+        for h in range(2):
+            for p in range(NPOS):
+                w_zero(p, h)
+                w_fill(p, h)
 
         graw = {}
         gd = {}
@@ -88,15 +102,23 @@ def tile_stdpconvinhibit_t_kernel(tc, in_spikes, weights, grad_out, out):
         bank = {}
         acc = {}
 
-        def load_g(s):
-            t = graw_pool.tile([P, 2 * 4 * CO], BF16, name="graw")
-            nc.sync.dma_start(out=t[:].rearrange("q (n e) -> q n e", n=2), in_=g_view[:, 2 * s : 2 * s + 2, :])
-            graw[s] = t
+        def load_t(n):
+            t = const.tile([P, 4 * CO], BF16, name="graw%d" % n)
+            nc.sync.dma_start(out=t[:], in_=gt_view[:, T_TILES.index(n), :])
+            graw[n] = t[:]
 
-        def load_g_tile(n):
-            if n == 0:
-                graw[0] = graw_pool.tile([P, 2 * 4 * CO], BF16, name="graw")
-            nc.sync.dma_start(out=graw[0][:, n * 4 * CO : (n + 1) * 4 * CO], in_=g_view[:, n, :])
+        def load_v(n, count=2):
+            i = VT_TILES.index(n)
+            t = const.tile([P, count * 8, 256], BF16, name="graw%d" % n)
+            for a in (0, 2, 1, 3):
+                for u in range(2):
+                    lo = (256 * u + 64 * a) * NPOS
+                    nc.sync.dma_start(
+                        out=t[32 * a + u : 32 * a + 32 : 2, :, :],
+                        in_=gv_view[:, 8 * i : 8 * (i + count), lo : lo + 256],
+                    )
+            for c in range(count):
+                graw[VT_TILES[i + c]] = t[:, 8 * c : 8 * c + 8, :].rearrange("q g e -> q (g e)")
 
         def load_w(p, h):
             nc.sync.dma_start(
@@ -117,30 +139,38 @@ def tile_stdpconvinhibit_t_kernel(tc, in_spikes, weights, grad_out, out):
             wt[(p, h)] = t
 
         def w_copy(p, h):
-            i, j = p // OW, p % OW
-            lo = w_base(p, h)
-            dst = wwords[:, lo + i * ROW : lo + (i + KW) * ROW].rearrange(
-                "q (y x c u) -> q y x c u", y=KW, x=IW, c=16, u=2
-            )
+            j = p % OW
+            dst = w_rows(p, h)[:, :, j : j + KW, :].rearrange("q y x (c u) -> q y x c u", u=2)
             nc.scalar.copy(
-                out=dst[:, :, j : j + KW, :, :],
+                out=dst,
                 in_=wt[(p, h)][:].rearrange("q (u c r v) -> q r v c u", u=2, c=16, r=KW, v=KW),
             )
 
         def w_quantise(p, h):
-            lo = rank[(p, h)] * HC * 4
-            nc.vector.quantize_mx(
-                out=wcod[(p, h)][:].bitcast(E4X4), scales=wsca[(p, h)][:], in_=wall[:, lo : lo + NB * 4]
-            )
+            calls = QUANT[p // OW]
+            base = calls[0][0]
+            for lo, n in calls:
+                nc.vector.quantize_mx(
+                    out=wcod[(p, h)][:, lo : lo + n].bitcast(E4X4),
+                    scales=wsca[(p, h)][:, lo : lo + n],
+                    in_=wpad[(p, h)][:, (lo - base) * 4 : (lo - base + n) * 4],
+                )
 
-        def deinterleave(n):
-            t = gd_pool.tile([P, 4 * CO], BF16, name="gd")
-            src = graw[n // 2][:, (n % 2) * 4 * CO : (n % 2 + 1) * 4 * CO]
-            nc.vector.tensor_copy(
-                out=t[:].rearrange("q (p c i) -> q c p i", p=NPOS, i=4),
-                in_=src.rearrange("q (c i p) -> q c p i", i=4, p=NPOS),
-            )
-            gd[n] = t
+        def deinterleave(n, part=None):
+            if part in (None, 0):
+                gd[n] = gd_pool.tile([P, 4 * CO], BF16, name="gd", align_bytes=64)
+            dst = gd[n][:].rearrange("q (p c i) -> q c p i", p=NPOS, i=4)
+            src = graw[n].rearrange("q (c i p) -> q c p i", i=4, p=NPOS)
+            if part is None:
+                nc.vector.tensor_copy(out=dst, in_=src)
+            else:
+                half = slice(part * 64, part * 64 + 64)
+                nc.scalar.copy(out=dst[:, half, :, :], in_=src[:, half, :, :])
+
+        def v_transpose(n):
+            grp = ggrp_pool.tile([P, 4 * NB], BF16, name="ggrp", align_bytes=64)
+            nc.vector.transpose(grp[:].bitcast(F32), gd[n][:].bitcast(F32))
+            gt[n] = grp
 
         def transposes(n):
             words = gd[n][:].bitcast(F32)
@@ -169,53 +199,54 @@ def tile_stdpconvinhibit_t_kernel(tc, in_spikes, weights, grad_out, out):
 
         def quantise(n):
             cod = gq_pool.tile([P, PAD + NB], U32, name="gcod", align_bytes=256)
-            sca = gq_pool.tile([P, NPOS * SLOT], U8, name="gsca", align_bytes=256)
-            for p in range(NPOS):
+            sca = gq_pool.tile([P, NB], U8, name="gsca", align_bytes=256)
+            nc.vector.quantize_mx(out=cod[:, PAD : PAD + NB].bitcast(E5X4), scales=sca[:], in_=gt[n][:])
+            gq[n] = (cod, sca)
+
+        def quantise2(n):
+            cod = gq_pool.tile([P, PAD + NB], U32, name="gcod", align_bytes=256)
+            sca = gq_pool.tile([P, NB], U8, name="gsca", align_bytes=256)
+            for ph in range(2):
                 nc.vector.quantize_mx(
-                    out=cod[:, PAD + p * P : PAD + (p + 1) * P].bitcast(E5X4),
-                    scales=sca[:, p * SLOT : p * SLOT + P],
-                    in_=gt[n][:, p * NB : (p + 1) * NB],
+                    out=cod[:, PAD + ph * 256 : PAD + (ph + 1) * 256].bitcast(E5X4),
+                    scales=sca[:, ph * 256 : (ph + 1) * 256],
+                    in_=gt[n][:, ph * 2 * NB : (ph + 1) * 2 * NB],
                 )
             gq[n] = (cod, sca)
 
-        def passes(n, h):
+        def passes(n, h, positions=range(NPOS)):
             cod, sca = gq[n]
-            t = psum_m.tile([P, NB], F32, name="mx")
-            for p in range(NPOS):
+            if positions[0] == 0:
+                bank[(n, h)] = psum_m.tile([P, NB], F32, name="mx")
+            for p in positions:
                 nc.tensor.matmul_mx(
-                    out=t[:],
+                    out=bank[(n, h)][:],
                     lhsT=cod[:, PAD + p * P : PAD + (p + 1) * P].bitcast(E5X4),
-                    lhsT_scale=sca[:, p * SLOT : p * SLOT + P],
+                    lhsT_scale=sca[:, p * P : (p + 1) * P],
                     rhs=wcod[(p, h)][:].bitcast(E4X4),
                     rhs_scale=wsca[(p, h)][:],
                     start=(p == 0),
                     stop=(p == NPOS - 1),
                 )
-            bank[(n, h)] = t
 
         def evacuate(n, h, on_vector=False):
-            if n % 2 == 0 and h == 0:
-                acc[n // 2] = acc_pool.tile([P, 2 * OUTC], F32, name="acc")
-            dst = acc[n // 2][:, (n % 2) * OUTC + h * HC : (n % 2) * OUTC + (h + 1) * HC].rearrange(
-                "q (c s) -> q c s", c=16
-            )
-            src = bank[(n, h)][:, JUNK:NB].rearrange("q (s c) -> q c s", c=16)
+            if h == 0:
+                acc[n] = acc_pool.tile([P, OUTC], F32, name="acc")
+            dst = acc[n][:, h * HC : (h + 1) * HC].rearrange("q (c s) -> q c s", c=16)
+            src = bank[(n, h)][:, FIRST : FIRST + HC].rearrange("q (s c) -> q c s", c=16)
             if on_vector:
                 nc.vector.tensor_copy(out=dst, in_=src)
             else:
                 nc.scalar.copy(out=dst, in_=src)
 
-        def store_pair(s):
-            nc.sync.dma_start(
-                out=o_view[:, 2 * s : 2 * s + 2, :], in_=acc[s][:].rearrange("q (n e) -> q n e", n=2)
-            )
+        def o_rows(n):
+            return ot_view[:, T_TILES.index(n), :] if n in T_TILES else ov_view[VT_TILES.index(n)]
 
         def store_half(n, h):
-            lo = (n % 2) * OUTC + h * HC
-            nc.sync.dma_start(out=o_view[:, n, h * HC : (h + 1) * HC], in_=acc[n // 2][:, lo : lo + HC])
+            nc.sync.dma_start(out=o_rows(n)[:, h * HC : (h + 1) * HC], in_=acc[n][:, h * HC : (h + 1) * HC])
 
         def store_one(n):
-            nc.sync.dma_start(out=o_view[:, n, :], in_=acc[n // 2][:, (n % 2) * OUTC : (n % 2 + 1) * OUTC])
+            nc.sync.dma_start(out=o_rows(n), in_=acc[n][:])
 
         def w_prepare(p, h, in_transpose_banks=False):
             if in_transpose_banks:
@@ -224,78 +255,99 @@ def tile_stdpconvinhibit_t_kernel(tc, in_spikes, weights, grad_out, out):
                 w_transpose(p, h, psum_m, "mx")
             w_copy(p, h)
 
-        def multiply(n, last=False):
-            passes(n, 0)
-            passes(n, 1)
-            evacuate(n, 0)
-            if last:
-                store_half(n, 0)
-            evacuate(n, 1, on_vector=last)
-            if last:
-                store_half(n, 1)
-
         load_w(0, 0)
-        load_g_tile(0)
+        load_t(0)
         load_w(1, 0)
         load_w(2, 0)
-        load_g_tile(1)
+        load_t(1)
         load_w(3, 0)
         for p in range(NPOS):
             load_w(p, 1)
-        for s in range(1, NG):
-            load_g(s)
-
+        load_t(2)
+        load_t(3)
+        load_t(4)
+        load_v(5)
+        load_t(6)
         w_prepare(0, 0)
         w_prepare(1, 0)
         w_prepare(2, 0)
         deinterleave(0)
         transposes(0)
         regroup(0)
-        w_prepare(3, 0)
         w_quantise(0, 0)
-        deinterleave(1)
         w_quantise(1, 0)
+        w_prepare(3, 0)
+        deinterleave(1)
         w_quantise(2, 0)
         quantise(0)
         w_quantise(3, 0)
         transposes(1)
         regroup(1)
-        for p in range(NPOS):
-            w_prepare(p, 1, in_transpose_banks=(p < 2))
+        w_prepare(0, 1, in_transpose_banks=True)
+        w_prepare(1, 1, in_transpose_banks=True)
         quantise(1)
-        for p in range(NPOS):
-            w_quantise(p, 1)
-        deinterleave(2)
-        deinterleave(3)
         passes(0, 0)
+        w_quantise(0, 1)
+        w_quantise(1, 1)
+        w_prepare(2, 1)
+        w_prepare(3, 1)
+        deinterleave(2)
         passes(1, 0)
-        passes(0, 1)
-        passes(1, 1)
         evacuate(0, 0)
         evacuate(1, 0)
-        evacuate(0, 1)
-        evacuate(1, 1)
-        store_pair(0)
+        w_quantise(2, 1)
+        w_quantise(3, 1)
+        passes(0, 1, (0, 1))
+        passes(1, 1, (0, 1))
         transposes(2)
-        transposes(3)
         regroup(2)
-        regroup(3)
+        deinterleave(3)
+        passes(0, 1, (2, 3))
+        passes(1, 1, (2, 3))
+        evacuate(0, 1)
+        store_one(0)
+        evacuate(1, 1)
+        store_one(1)
         quantise(2)
+        transposes(3)
+        regroup(3)
         deinterleave(4)
-        multiply(2)
-        for n in range(3, NT - 2, 2):
-            deinterleave(n + 2)
-            transposes(n + 1)
-            transposes(n + 2)
-            quantise(n)
-            regroup(n + 1)
-            if n + 3 < NT:
-                deinterleave(n + 3)
-            quantise(n + 1)
-            regroup(n + 2)
-            multiply(n)
-            store_pair(n // 2)
-            multiply(n + 1)
-        quantise(NT - 1)
-        store_one(NT - 2)
-        multiply(NT - 1, last=True)
+        deinterleave(5)
+        quantise(3)
+        for n in range(2, NT, 2):
+            nxt = [m for m in (n + 2, n + 3) if m < NT]
+            ahead = [m for m in (n + 4, n + 5) if m < NT]
+            for m in nxt:
+                if m in T_TILES:
+                    transposes(m)
+            for m in nxt:
+                if m in T_TILES:
+                    regroup(m)
+            for m in ahead:
+                if m in T_TILES:
+                    deinterleave(m)
+            if n + 6 < NT:
+                load_t(n + 6)
+            if n + 7 in VT_TILES and VT_TILES.index(n + 7) % 2 == 0:
+                load_v(n + 7)
+            if nxt:
+                quantise(n + 2)
+                if n + 3 in VT_TILES:
+                    v_transpose(n + 3)
+            passes(n, 0)
+            evacuate(n, 0)
+            if n + 5 in VT_TILES:
+                deinterleave(n + 5, 0)
+            passes(n, 1)
+            evacuate(n, 1)
+            store_one(n)
+            if n + 5 in VT_TILES:
+                deinterleave(n + 5, 1)
+            passes(n + 1, 0)
+            evacuate(n + 1, 0, on_vector=True)
+            store_half(n + 1, 0)
+            passes(n + 1, 1)
+            evacuate(n + 1, 1)
+            store_half(n + 1, 1)
+            if nxt:
+                quantise(n + 3)

@@ -23,7 +23,8 @@ NB = 512
 FLOPS = 2 * NPOS * B * CO * CI * KW * KW
 BYTES = 2 * B * CO * NPOS + 2 * NPOS * CI * KW * KW * CO + 4 * B * OUTC
 PAD = 32
-VT_TILES = [5, 7, 9, 11, 13, 15]
+AHEAD = 6
+VT_TILES = [5,6,8,9,11,12,14,15]
 T_TILES = [n for n in range(NT) if n not in VT_TILES]
 NTT = len(T_TILES)
 FIRST = 48
@@ -37,7 +38,7 @@ def tile_stdpconvinhibit_t_kernel(tc, in_spikes, weights, grad_out, out):
     split = P * NTT
     gt_view = grad_out[0:split].rearrange("(q n) k i j -> q n (k i j)", n=NTT)
     ot_view = out[0:split].rearrange("(q n) c h w -> q n (c h w)", n=NTT)
-    gv_view = grad_out[split:B].rearrange("(g b) k i j -> b g (k i j)", b=16)
+    gv_view = grad_out[split:B].rearrange("(g b) (u k) i j -> (b u) g (k i j)", b=16, u=2)
     ov_view = out[split:B].rearrange("(n q) c h w -> n q (c h w)", q=P)
     w_view = weights.rearrange("i j c u v k -> (i j c u v) k").rearrange("(n q) k -> q n k", q=P)
 
@@ -110,12 +111,11 @@ def tile_stdpconvinhibit_t_kernel(tc, in_spikes, weights, grad_out, out):
         def load_v(n, count=2):
             i = VT_TILES.index(n)
             t = const.tile([P, count * 8, 256], BF16, name="graw%d" % n)
-            for a in (0, 2, 1, 3):
-                for u in range(2):
-                    lo = (256 * u + 64 * a) * NPOS
-                    nc.sync.dma_start(
-                        out=t[32 * a + u : 32 * a + 32 : 2, :, :],
-                        in_=gv_view[:, 8 * i : 8 * (i + count), lo : lo + 256],
+            for a in range(2):
+                for queue, quarter in ((nc.sync, a), (nc.scalar, a + 2)):
+                    queue.dma_start(
+                        out=t[32 * quarter : 32 * quarter + 32, :, :],
+                        in_=gv_view[:, 8 * i : 8 * (i + count), 256 * quarter : 256 * quarter + 256],
                     )
             for c in range(count):
                 graw[VT_TILES[i + c]] = t[:, 8 * c : 8 * c + 8, :].rearrange("q g e -> q (g e)")
@@ -255,6 +255,12 @@ def tile_stdpconvinhibit_t_kernel(tc, in_spikes, weights, grad_out, out):
                 w_transpose(p, h, psum_m, "mx")
             w_copy(p, h)
 
+        def load_ahead(n):
+            if n in T_TILES:
+                load_t(n)
+            elif n in VT_TILES and VT_TILES.index(n) % 2 == 0:
+                load_v(n)
+
         load_w(0, 0)
         load_t(0)
         load_w(1, 0)
@@ -266,8 +272,6 @@ def tile_stdpconvinhibit_t_kernel(tc, in_spikes, weights, grad_out, out):
         load_t(2)
         load_t(3)
         load_t(4)
-        load_v(5)
-        load_t(6)
         w_prepare(0, 0)
         w_prepare(1, 0)
         w_prepare(2, 0)
@@ -285,6 +289,7 @@ def tile_stdpconvinhibit_t_kernel(tc, in_spikes, weights, grad_out, out):
         regroup(1)
         w_prepare(0, 1, in_transpose_banks=True)
         w_prepare(1, 1, in_transpose_banks=True)
+        load_ahead(5)
         quantise(1)
         passes(0, 0)
         w_quantise(0, 1)
@@ -308,46 +313,33 @@ def tile_stdpconvinhibit_t_kernel(tc, in_spikes, weights, grad_out, out):
         store_one(0)
         evacuate(1, 1)
         store_one(1)
+        load_ahead(7)
         quantise(2)
-        transposes(3)
-        regroup(3)
+        if 3 in VT_TILES:
+            v_transpose(3)
+        else:
+            transposes(3)
+            regroup(3)
         deinterleave(4)
-        deinterleave(5)
-        quantise(3)
-        for n in range(2, NT, 2):
-            nxt = [m for m in (n + 2, n + 3) if m < NT]
-            ahead = [m for m in (n + 4, n + 5) if m < NT]
-            for m in nxt:
-                if m in T_TILES:
-                    transposes(m)
-            for m in nxt:
-                if m in T_TILES:
-                    regroup(m)
-            for m in ahead:
-                if m in T_TILES:
-                    deinterleave(m)
-            if n + 6 < NT:
-                load_t(n + 6)
-            if n + 7 in VT_TILES and VT_TILES.index(n + 7) % 2 == 0:
-                load_v(n + 7)
-            if nxt:
-                quantise(n + 2)
-                if n + 3 in VT_TILES:
-                    v_transpose(n + 3)
+        for n in range(2, NT):
+            if n + 2 in T_TILES:
+                transposes(n + 2)
+                regroup(n + 2)
+            load_ahead(n + AHEAD)
+            if n + 1 < NT:
+                quantise(n + 1)
+            if n + 2 in VT_TILES:
+                v_transpose(n + 2)
+            if n + 3 < NT:
+                deinterleave(n + 3)
+            last = n == NT - 1
             passes(n, 0)
             evacuate(n, 0)
-            if n + 5 in VT_TILES:
-                deinterleave(n + 5, 0)
+            if last:
+                store_half(n, 0)
             passes(n, 1)
-            evacuate(n, 1)
-            store_one(n)
-            if n + 5 in VT_TILES:
-                deinterleave(n + 5, 1)
-            passes(n + 1, 0)
-            evacuate(n + 1, 0, on_vector=True)
-            store_half(n + 1, 0)
-            passes(n + 1, 1)
-            evacuate(n + 1, 1)
-            store_half(n + 1, 1)
-            if nxt:
-                quantise(n + 3)
+            evacuate(n, 1, on_vector=last)
+            if last:
+                store_half(n, 1)
+            else:
+                store_one(n)

@@ -23,7 +23,9 @@ NB = 512
 FLOPS = 2 * NPOS * B * CO * CI * KW * KW
 BYTES = 2 * B * CO * NPOS + 2 * NPOS * CI * KW * KW * CO + 4 * B * OUTC
 PAD = 32
-AHEAD = 6
+S1 = 5
+S2 = 4
+S_TILES = []
 VT_TILES = [5,6,8,9,11,12,14,15]
 T_TILES = [n for n in range(NT) if n not in VT_TILES]
 NTT = len(T_TILES)
@@ -44,10 +46,10 @@ def tile_stdpconvinhibit_t_kernel(tc, in_spikes, weights, grad_out, out):
 
     with ExitStack() as ctx:
         const = ctx.enter_context(tc.tile_pool(name="const", bufs=1))
-        gd_pool = ctx.enter_context(tc.tile_pool(name="gd", bufs=6))
+        gd_pool = ctx.enter_context(tc.tile_pool(name="gd", bufs=8))
         ggrp_pool = ctx.enter_context(tc.tile_pool(name="ggrp", bufs=4))
         gq_pool = ctx.enter_context(tc.tile_pool(name="gq", bufs=6))
-        acc_pool = ctx.enter_context(tc.tile_pool(name="acc", bufs=6))
+        acc_pool = ctx.enter_context(tc.tile_pool(name="acc", bufs=10))
         psum_t = ctx.enter_context(tc.psum_pool(name="psum_t", bufs=4))
         psum_m = ctx.enter_context(tc.psum_pool(name="psum_m", bufs=4))
         ctx.enter_context(tc.manual_schedule())
@@ -111,12 +113,11 @@ def tile_stdpconvinhibit_t_kernel(tc, in_spikes, weights, grad_out, out):
         def load_v(n, count=2):
             i = VT_TILES.index(n)
             t = const.tile([P, count * 8, 256], BF16, name="graw%d" % n)
-            for a in range(2):
-                for queue, quarter in ((nc.sync, a), (nc.scalar, a + 2)):
-                    queue.dma_start(
-                        out=t[32 * quarter : 32 * quarter + 32, :, :],
-                        in_=gv_view[:, 8 * i : 8 * (i + count), 256 * quarter : 256 * quarter + 256],
-                    )
+            for a in (0, 2, 1, 3):
+                nc.sync.dma_start(
+                    out=t[32 * a : 32 * a + 32, :, :],
+                    in_=gv_view[:, 8 * i : 8 * (i + count), 256 * a : 256 * a + 256],
+                )
             for c in range(count):
                 graw[VT_TILES[i + c]] = t[:, 8 * c : 8 * c + 8, :].rearrange("q g e -> q (g e)")
 
@@ -156,16 +157,17 @@ def tile_stdpconvinhibit_t_kernel(tc, in_spikes, weights, grad_out, out):
                     in_=wpad[(p, h)][:, (lo - base) * 4 : (lo - base + n) * 4],
                 )
 
-        def deinterleave(n, part=None):
-            if part in (None, 0):
+        def deinterleave(n, quarters=None):
+            if quarters is None or quarters[0] == 0:
                 gd[n] = gd_pool.tile([P, 4 * CO], BF16, name="gd", align_bytes=64)
             dst = gd[n][:].rearrange("q (p c i) -> q c p i", p=NPOS, i=4)
             src = graw[n].rearrange("q (c i p) -> q c p i", i=4, p=NPOS)
-            if part is None:
+            if quarters is None:
                 nc.vector.tensor_copy(out=dst, in_=src)
             else:
-                half = slice(part * 64, part * 64 + 64)
-                nc.scalar.copy(out=dst[:, half, :, :], in_=src[:, half, :, :])
+                for r in quarters:
+                    part = slice(r * 32, r * 32 + 32)
+                    nc.scalar.copy(out=dst[:, part, :, :], in_=src[:, part, :, :])
 
         def v_transpose(n):
             grp = ggrp_pool.tile([P, 4 * NB], BF16, name="ggrp", align_bytes=64)
@@ -255,12 +257,6 @@ def tile_stdpconvinhibit_t_kernel(tc, in_spikes, weights, grad_out, out):
                 w_transpose(p, h, psum_m, "mx")
             w_copy(p, h)
 
-        def load_ahead(n):
-            if n in T_TILES:
-                load_t(n)
-            elif n in VT_TILES and VT_TILES.index(n) % 2 == 0:
-                load_v(n)
-
         load_w(0, 0)
         load_t(0)
         load_w(1, 0)
@@ -269,9 +265,12 @@ def tile_stdpconvinhibit_t_kernel(tc, in_spikes, weights, grad_out, out):
         load_w(3, 0)
         for p in range(NPOS):
             load_w(p, 1)
-        load_t(2)
-        load_t(3)
-        load_t(4)
+        for n in range(2, NT):
+            if n in T_TILES:
+                load_t(n)
+            elif VT_TILES.index(n) % 2 == 0:
+                load_v(n)
+
         w_prepare(0, 0)
         w_prepare(1, 0)
         w_prepare(2, 0)
@@ -289,7 +288,6 @@ def tile_stdpconvinhibit_t_kernel(tc, in_spikes, weights, grad_out, out):
         regroup(1)
         w_prepare(0, 1, in_transpose_banks=True)
         w_prepare(1, 1, in_transpose_banks=True)
-        load_ahead(5)
         quantise(1)
         passes(0, 0)
         w_quantise(0, 1)
@@ -313,7 +311,6 @@ def tile_stdpconvinhibit_t_kernel(tc, in_spikes, weights, grad_out, out):
         store_one(0)
         evacuate(1, 1)
         store_one(1)
-        load_ahead(7)
         quantise(2)
         if 3 in VT_TILES:
             v_transpose(3)
@@ -325,21 +322,21 @@ def tile_stdpconvinhibit_t_kernel(tc, in_spikes, weights, grad_out, out):
             if n + 2 in T_TILES:
                 transposes(n + 2)
                 regroup(n + 2)
-            load_ahead(n + AHEAD)
             if n + 1 < NT:
                 quantise(n + 1)
             if n + 2 in VT_TILES:
                 v_transpose(n + 2)
-            if n + 3 < NT:
+            if n + 3 < NT and n + 3 not in S_TILES:
                 deinterleave(n + 3)
             last = n == NT - 1
-            passes(n, 0)
-            evacuate(n, 0)
-            if last:
-                store_half(n, 0)
-            passes(n, 1)
-            evacuate(n, 1, on_vector=last)
-            if last:
-                store_half(n, 1)
-            else:
+            for h in range(2):
+                passes(n, h)
+                evacuate(n, h, on_vector=(last and h == 1))
+                if n + S1 in S_TILES:
+                    deinterleave(n + S1, (h,))
+                if n + S2 in S_TILES:
+                    deinterleave(n + S2, (2 + h,))
+                if last:
+                    store_half(n, h)
+            if not last:
                 store_one(n)

@@ -25,8 +25,8 @@ BYTES = 2 * B * CO * NPOS + 2 * NPOS * CI * KW * KW * CO + 4 * B * OUTC
 PAD = 32
 S1 = 5
 S2 = 4
-S_TILES = []
-VT_TILES = [5,6,8,9,11,12,14,15]
+S_TILES = [7,9,11,13,15]
+VT_TILES = [5,6,7,8,9,10,11,12,13,14,15]
 T_TILES = [n for n in range(NT) if n not in VT_TILES]
 NTT = len(T_TILES)
 FIRST = 48
@@ -54,6 +54,8 @@ def tile_stdpconvinhibit_t_kernel(tc, in_spikes, weights, grad_out, out):
         psum_m = ctx.enter_context(tc.psum_pool(name="psum_m", bufs=4))
         ctx.enter_context(tc.manual_schedule())
 
+        zeros = const.tile([P, NB], BF16, name="zeros")
+        nc.vector.memset(zeros[:].bitcast(I32), 0)
         ident = const.tile([P, P], F32, name="ident")
         make_identity(nc, ident[:])
 
@@ -110,7 +112,7 @@ def tile_stdpconvinhibit_t_kernel(tc, in_spikes, weights, grad_out, out):
             nc.sync.dma_start(out=t[:], in_=gt_view[:, T_TILES.index(n), :])
             graw[n] = t[:]
 
-        def load_v(n, count=2):
+        def load_v(n, count=1):
             i = VT_TILES.index(n)
             t = const.tile([P, count * 8, 256], BF16, name="graw%d" % n)
             for a in (0, 2, 1, 3):
@@ -127,9 +129,11 @@ def tile_stdpconvinhibit_t_kernel(tc, in_spikes, weights, grad_out, out):
                 in_=w_view[:, 4 * p + 2 * h : 4 * p + 2 * h + 2, :],
             )
 
-        def w_transpose(p, h, pool, tag):
+        def w_transpose(p, h, pool, tag, warm):
             words = wraw[(p, h)][:].bitcast(F32)
             t = pool.tile([P, NB], F32, name=tag)
+            for r in range(warm):
+                nc.tensor.matmul(t[:], lhsT=zeros[:, 0:P], rhs=zeros[:], start=True, stop=True)
             for al in range(2):
                 for u in range(2):
                     nc.tensor.transpose(
@@ -250,11 +254,11 @@ def tile_stdpconvinhibit_t_kernel(tc, in_spikes, weights, grad_out, out):
         def store_one(n):
             nc.sync.dma_start(out=o_rows(n), in_=acc[n][:])
 
-        def w_prepare(p, h, in_transpose_banks=False):
+        def w_prepare(p, h, in_transpose_banks=False, warm=0):
             if in_transpose_banks:
-                w_transpose(p, h, psum_t, "gt")
+                w_transpose(p, h, psum_t, "gt", warm)
             else:
-                w_transpose(p, h, psum_m, "mx")
+                w_transpose(p, h, psum_m, "mx", warm)
             w_copy(p, h)
 
         load_w(0, 0)
@@ -268,18 +272,18 @@ def tile_stdpconvinhibit_t_kernel(tc, in_spikes, weights, grad_out, out):
         for n in range(2, NT):
             if n in T_TILES:
                 load_t(n)
-            elif VT_TILES.index(n) % 2 == 0:
+            elif True:
                 load_v(n)
 
-        w_prepare(0, 0)
-        w_prepare(1, 0)
-        w_prepare(2, 0)
+        w_prepare(0, 0, warm=4)
+        w_prepare(1, 0, warm=2)
+        w_prepare(2, 0, warm=0)
         deinterleave(0)
         transposes(0)
         regroup(0)
         w_quantise(0, 0)
         w_quantise(1, 0)
-        w_prepare(3, 0)
+        w_prepare(3, 0, warm=2)
         deinterleave(1)
         w_quantise(2, 0)
         quantise(0)

@@ -49,7 +49,7 @@ def tile_stdpconvinhibit_t_kernel(tc, in_spikes, weights, grad_out, out):
         gd_pool = ctx.enter_context(tc.tile_pool(name="gd", bufs=8))
         ggrp_pool = ctx.enter_context(tc.tile_pool(name="ggrp", bufs=4))
         gq_pool = ctx.enter_context(tc.tile_pool(name="gq", bufs=6))
-        acc_pool = ctx.enter_context(tc.tile_pool(name="acc", bufs=10))
+        acc_pool = ctx.enter_context(tc.tile_pool(name="acc", bufs=12))
         psum_t = ctx.enter_context(tc.psum_pool(name="psum_t", bufs=4))
         psum_m = ctx.enter_context(tc.psum_pool(name="psum_m", bufs=4))
         ctx.enter_context(tc.manual_schedule())
@@ -161,16 +161,16 @@ def tile_stdpconvinhibit_t_kernel(tc, in_spikes, weights, grad_out, out):
                     in_=wpad[(p, h)][:, (lo - base) * 4 : (lo - base + n) * 4],
                 )
 
-        def deinterleave(n, quarters=None):
-            if quarters is None or quarters[0] == 0:
+        def deinterleave(n, halves=None):
+            if halves is None or halves[0] == 0:
                 gd[n] = gd_pool.tile([P, 4 * CO], BF16, name="gd", align_bytes=64)
             dst = gd[n][:].rearrange("q (p c i) -> q c p i", p=NPOS, i=4)
             src = graw[n].rearrange("q (c i p) -> q c p i", i=4, p=NPOS)
-            if quarters is None:
+            if halves is None:
                 nc.vector.tensor_copy(out=dst, in_=src)
             else:
-                for r in quarters:
-                    part = slice(r * 32, r * 32 + 32)
+                for r in halves:
+                    part = slice(r * 64, r * 64 + 64)
                     nc.scalar.copy(out=dst[:, part, :, :], in_=src[:, part, :, :])
 
         def v_transpose(n):
@@ -235,11 +235,12 @@ def tile_stdpconvinhibit_t_kernel(tc, in_spikes, weights, grad_out, out):
                     stop=(p == NPOS - 1),
                 )
 
-        def evacuate(n, h, on_vector=False):
+        def evacuate(n, h, channels=16, first=0, on_vector=False):
             if h == 0:
                 acc[n] = acc_pool.tile([P, OUTC], F32, name="acc")
-            dst = acc[n][:, h * HC : (h + 1) * HC].rearrange("q (c s) -> q c s", c=16)
-            src = bank[(n, h)][:, FIRST : FIRST + HC].rearrange("q (s c) -> q c s", c=16)
+            lo = h * HC + first * IH * IW
+            dst = acc[n][:, lo : lo + channels * IH * IW].rearrange("q (c s) -> q c s", c=channels)
+            src = bank[(n, h)][:, FIRST : FIRST + HC].rearrange("q (s c) -> q c s", c=16)[:, first : first + channels, :]
             if on_vector:
                 nc.vector.tensor_copy(out=dst, in_=src)
             else:
@@ -248,8 +249,8 @@ def tile_stdpconvinhibit_t_kernel(tc, in_spikes, weights, grad_out, out):
         def o_rows(n):
             return ot_view[:, T_TILES.index(n), :] if n in T_TILES else ov_view[VT_TILES.index(n)]
 
-        def store_half(n, h):
-            nc.sync.dma_start(out=o_rows(n)[:, h * HC : (h + 1) * HC], in_=acc[n][:, h * HC : (h + 1) * HC])
+        def store_part(n, lo, hi):
+            nc.sync.dma_start(out=o_rows(n)[:, lo:hi], in_=acc[n][:, lo:hi])
 
         def store_one(n):
             nc.sync.dma_start(out=o_rows(n), in_=acc[n][:])
@@ -302,25 +303,20 @@ def tile_stdpconvinhibit_t_kernel(tc, in_spikes, weights, grad_out, out):
         passes(1, 0)
         evacuate(0, 0)
         evacuate(1, 0)
-        w_quantise(2, 1)
-        w_quantise(3, 1)
-        passes(0, 1, (0, 1))
-        passes(1, 1, (0, 1))
         transposes(2)
         regroup(2)
-        deinterleave(3)
-        passes(0, 1, (2, 3))
-        passes(1, 1, (2, 3))
+        w_quantise(2, 1)
+        w_quantise(3, 1)
+        passes(0, 1)
         evacuate(0, 1)
         store_one(0)
+        deinterleave(3)
+        transposes(3)
+        quantise(2)
+        regroup(3)
+        passes(1, 1)
         evacuate(1, 1)
         store_one(1)
-        quantise(2)
-        if 3 in VT_TILES:
-            v_transpose(3)
-        else:
-            transposes(3)
-            regroup(3)
         deinterleave(4)
         for n in range(2, NT):
             if n + 2 in T_TILES:
@@ -332,15 +328,17 @@ def tile_stdpconvinhibit_t_kernel(tc, in_spikes, weights, grad_out, out):
                 v_transpose(n + 2)
             if n + 3 < NT and n + 3 not in S_TILES:
                 deinterleave(n + 3)
-            last = n == NT - 1
-            for h in range(2):
-                passes(n, h)
-                evacuate(n, h, on_vector=(last and h == 1))
-                if n + S1 in S_TILES:
-                    deinterleave(n + S1, (h,))
-                if n + S2 in S_TILES:
-                    deinterleave(n + S2, (2 + h,))
-                if last:
-                    store_half(n, h)
-            if not last:
+            passes(n, 0)
+            evacuate(n, 0)
+            if n + S1 in S_TILES:
+                deinterleave(n + S1, (0,))
+            if n + S2 in S_TILES:
+                deinterleave(n + S2, (1,))
+            passes(n, 1)
+            if n < NT - 1:
+                evacuate(n, 1)
                 store_one(n)
+        store_part(NT - 1, 0, HC)
+        for first in (0, 8):
+            evacuate(NT - 1, 1, channels=8, first=first, on_vector=True)
+            store_part(NT - 1, HC + first * IH * IW, HC + (first + 8) * IH * IW)

@@ -23,9 +23,9 @@ NB = 512
 FLOPS = 2 * NPOS * B * CO * CI * KW * KW
 BYTES = 2 * B * CO * NPOS + 2 * NPOS * CI * KW * KW * CO + 4 * B * OUTC
 PAD = 32
-S1 = 5
+S1 = 4
 S2 = 4
-S_TILES = [7,9,11,13,15]
+S_TILES = [8,10,12,14]
 VT_TILES = [5,6,7,8,9,10,11,12,13,14,15]
 T_TILES = [n for n in range(NT) if n not in VT_TILES]
 NTT = len(T_TILES)
@@ -273,7 +273,7 @@ def tile_stdpconvinhibit_t_kernel(tc, in_spikes, weights, grad_out, out):
         for n in range(2, NT):
             if n in T_TILES:
                 load_t(n)
-            elif True:
+            else:
                 load_v(n)
 
         w_prepare(0, 0, warm=4)
@@ -332,12 +332,12 @@ def tile_stdpconvinhibit_t_kernel(tc, in_spikes, weights, grad_out, out):
             evacuate(n, 0)
             if n + S1 in S_TILES:
                 deinterleave(n + S1, (0,))
-            if n + S2 in S_TILES:
-                deinterleave(n + S2, (1,))
             passes(n, 1)
             if n < NT - 1:
                 evacuate(n, 1)
                 store_one(n)
+            if n + S1 in S_TILES:
+                deinterleave(n + S1, (1,))
         store_part(NT - 1, 0, HC)
         for first in (0, 8):
             evacuate(NT - 1, 1, channels=8, first=first, on_vector=True)

@@ -26,7 +26,7 @@ PAD = 32
 S1 = 4
 S2 = 4
 S_TILES = [8,10,12,14]
-VT_TILES = [5,6,7,8,9,10,11,12,13,14,15]
+VT_TILES = [6,7,8,9,10,11,12,13,14,15]
 T_TILES = [n for n in range(NT) if n not in VT_TILES]
 NTT = len(T_TILES)
 FIRST = 48

from contextlib import ExitStack

import concourse.mybir as mybir
from concourse.masks import make_identity

F32 = mybir.dt.float32
BF16 = mybir.dt.bfloat16
U32 = mybir.dt.uint32
U8 = mybir.dt.uint8
I32 = mybir.dt.int32
E5X4 = mybir.dt.float8_e5m2_x4
E4X4 = mybir.dt.float8_e4m3fn_x4

P = 128
B, CI, CO, OH, OW, KW = 2048, 32, 512, 2, 2, 4
IH, IW = 5, 5
NPOS = OH * OW
NT = B // P
OUTC = CI * IH * IW
HC = OUTC // 2
NB = 512

FLOPS = 2 * NPOS * B * CO * CI * KW * KW
BYTES = 2 * B * CO * NPOS + 2 * NPOS * CI * KW * KW * CO + 4 * B * OUTC
PAD = 32
S1 = 4
S2 = 4
S_TILES = [8,10,12,14]
VT_TILES = [6,7,8,9,10,11,12,13,14,15]
T_TILES = [n for n in range(NT) if n not in VT_TILES]
NTT = len(T_TILES)
FIRST = 48
PIX = 16
QUANT = {0: ((0, 256), (256, 128)), 1: ((128, 256), (384, 64))}
FILL = {0: ((384, 512),), 1: ((0, 128), (448, 512))}


def tile_stdpconvinhibit_t_kernel(tc, in_spikes, weights, grad_out, out):
    nc = tc.nc
    split = P * NTT
    gt_view = grad_out[0:split].rearrange("(q n) k i j -> q n (k i j)", n=NTT)
    ot_view = out[0:split].rearrange("(q n) c h w -> q n (c h w)", n=NTT)
    gv_view = grad_out[split:B].rearrange("(g b) (u k) i j -> (b u) g (k i j)", b=16, u=2)
    ov_view = out[split:B].rearrange("(n q) c h w -> n q (c h w)", q=P)
    w_view = weights.rearrange("i j c u v k -> (i j c u v) k").rearrange("(n q) k -> q n k", q=P)

    with ExitStack() as ctx:
        const = ctx.enter_context(tc.tile_pool(name="const", bufs=1))
        gd_pool = ctx.enter_context(tc.tile_pool(name="gd", bufs=8))
        ggrp_pool = ctx.enter_context(tc.tile_pool(name="ggrp", bufs=4))
        gq_pool = ctx.enter_context(tc.tile_pool(name="gq", bufs=6))
        acc_pool = ctx.enter_context(tc.tile_pool(name="acc", bufs=12))
        psum_t = ctx.enter_context(tc.psum_pool(name="psum_t", bufs=4))
        psum_m = ctx.enter_context(tc.psum_pool(name="psum_m", bufs=4))
        ctx.enter_context(tc.manual_schedule())

        zeros = const.tile([P, NB], BF16, name="zeros")
        nc.vector.memset(zeros[:].bitcast(I32), 0)
        ident = const.tile([P, P], F32, name="ident")
        make_identity(nc, ident[:])

        keys = [(p, h) for p in range(NPOS) for h in range(2)]
        wraw = dict((k, const.tile([P, 2 * CO], BF16, name="wraw%d%d" % k)) for k in keys)
        wcod = dict((k, const.tile([P, NB], U32, name="wcod%d%d" % k, align_bytes=256)) for k in keys)
        wsca = dict((k, const.tile([P, NB], U8, name="wsca%d%d" % k, align_bytes=256)) for k in keys)
        wpad = dict(
            (k, const.tile([P, 4 * sum(w for s, w in QUANT[k[0] // OW])], BF16, name="wpad%d%d" % k, align_bytes=64))
            for k in keys
        )

        def w_rows(p, h):
            i = p // OW
            lo = (FIRST + i * IW * PIX - QUANT[i][0][0]) * 2
            words = wpad[(p, h)][:].bitcast(F32)[:, lo : lo + KW * IW * PIX * 2]
            return words.rearrange("q (y x e) -> q y x e", y=KW, x=IW)

        def w_zero(p, h):
            i, j = p // OW, p % OW
            ints = wpad[(p, h)][:].bitcast(I32)
            lo = (FIRST + i * IW * PIX - QUANT[i][0][0]) * 2
            hi = lo + KW * IW * PIX * 2
            end = 2 * sum(w for s, w in QUANT[i])
            if lo > 0:
                nc.vector.memset(ints[:, 0:lo], 0)
            if hi < end:
                nc.vector.memset(ints[:, hi:end], 0)
            rows = ints[:, lo:hi].rearrange("q (y x e) -> q y x e", y=KW, x=IW)
            x0 = (IW - 1) * (1 - j)
            nc.vector.memset(rows[:, :, x0, :], 0)

        def w_fill(p, h):
            scales = wsca[(p, h)][:].bitcast(I32)
            for lo, hi in FILL[p // OW]:
                nc.gpsimd.memset(wcod[(p, h)][:, lo:hi], 0)
                nc.gpsimd.memset(scales[:, lo // 4 : hi // 4], 0)

        for h in range(2):
            for p in range(NPOS):
                w_zero(p, h)
                w_fill(p, h)

        graw = {}
        gd = {}
        gt = {}
        gq = {}
        wt = {}
        bank = {}
        acc = {}

        def load_t(n):
            t = const.tile([P, 4 * CO], BF16, name="graw%d" % n)
            nc.sync.dma_start(out=t[:], in_=gt_view[:, T_TILES.index(n), :])
            graw[n] = t[:]

        def load_v(n, count=1):
            i = VT_TILES.index(n)
            t = const.tile([P, count * 8, 256], BF16, name="graw%d" % n)
            for a in (0, 2, 1, 3):
                nc.sync.dma_start(
                    out=t[32 * a : 32 * a + 32, :, :],
                    in_=gv_view[:, 8 * i : 8 * (i + count), 256 * a : 256 * a + 256],
                )
            for c in range(count):
                graw[VT_TILES[i + c]] = t[:, 8 * c : 8 * c + 8, :].rearrange("q g e -> q (g e)")

        def load_w(p, h):
            nc.sync.dma_start(
                out=wraw[(p, h)][:].rearrange("q (n k) -> q n k", n=2),
                in_=w_view[:, 4 * p + 2 * h : 4 * p + 2 * h + 2, :],
            )

        def w_transpose(p, h, pool, tag, warm):
            words = wraw[(p, h)][:].bitcast(F32)
            t = pool.tile([P, NB], F32, name=tag)
            for r in range(warm):
                nc.tensor.matmul(t[:], lhsT=zeros[:, 0:P], rhs=zeros[:], start=True, stop=True)
            for al in range(2):
                for u in range(2):
                    nc.tensor.transpose(
                        t[:, u * 256 + al * P : u * 256 + (al + 1) * P],
                        words[:, al * 256 + u * P : al * 256 + (u + 1) * P],
                        ident[:],
                    )
            wt[(p, h)] = t

        def w_copy(p, h):
            j = p % OW
            dst = w_rows(p, h)[:, :, j : j + KW, :].rearrange("q y x (c u) -> q y x c u", u=2)
            nc.scalar.copy(
                out=dst,
                in_=wt[(p, h)][:].rearrange("q (u c r v) -> q r v c u", u=2, c=16, r=KW, v=KW),
            )

        def w_quantise(p, h):
            calls = QUANT[p // OW]
            base = calls[0][0]
            for lo, n in calls:
                nc.vector.quantize_mx(
                    out=wcod[(p, h)][:, lo : lo + n].bitcast(E4X4),
                    scales=wsca[(p, h)][:, lo : lo + n],
                    in_=wpad[(p, h)][:, (lo - base) * 4 : (lo - base + n) * 4],
                )

        def deinterleave(n, halves=None):
            if halves is None or halves[0] == 0:
                gd[n] = gd_pool.tile([P, 4 * CO], BF16, name="gd", align_bytes=64)
            dst = gd[n][:].rearrange("q (p c i) -> q c p i", p=NPOS, i=4)
            src = graw[n].rearrange("q (c i p) -> q c p i", i=4, p=NPOS)
            if halves is None:
                nc.vector.tensor_copy(out=dst, in_=src)
            else:
                for r in halves:
                    part = slice(r * 64, r * 64 + 64)
                    nc.scalar.copy(out=dst[:, part, :, :], in_=src[:, part, :, :])

        def v_transpose(n):
            grp = ggrp_pool.tile([P, 4 * NB], BF16, name="ggrp", align_bytes=64)
            nc.vector.transpose(grp[:].bitcast(F32), gd[n][:].bitcast(F32))
            gt[n] = grp

        def transposes(n):
            words = gd[n][:].bitcast(F32)
            banks = []
            for ph in range(2):
                t = psum_t.tile([P, NB], F32, name="gt")
                for pl in range(2):
                    for u in range(2):
                        nc.tensor.transpose(
                            t[:, (pl * 2 + u) * P : (pl * 2 + u + 1) * P],
                            words[:, (2 * ph + pl) * 256 + u * P : (2 * ph + pl) * 256 + (u + 1) * P],
                            ident[:],
                        )
                banks.append(t)
            gt[n] = banks

        def regroup(n):
            grp = ggrp_pool.tile([P, 4 * NB], BF16, name="ggrp", align_bytes=64)
            gw = grp[:].bitcast(F32)
            for ph in range(2):
                nc.scalar.copy(
                    out=gw[:, ph * NB : (ph + 1) * NB].rearrange("q (p b u) -> q p b u", p=2, u=2),
                    in_=gt[n][ph][:].rearrange("q (p u b) -> q p b u", p=2, u=2),
                )
            gt[n] = grp

        def quantise(n):
            cod = gq_pool.tile([P, PAD + NB], U32, name="gcod", align_bytes=256)
            sca = gq_pool.tile([P, NB], U8, name="gsca", align_bytes=256)
            nc.vector.quantize_mx(out=cod[:, PAD : PAD + NB].bitcast(E5X4), scales=sca[:], in_=gt[n][:])
            gq[n] = (cod, sca)

        def quantise2(n):
            cod = gq_pool.tile([P, PAD + NB], U32, name="gcod", align_bytes=256)
            sca = gq_pool.tile([P, NB], U8, name="gsca", align_bytes=256)
            for ph in range(2):
                nc.vector.quantize_mx(
                    out=cod[:, PAD + ph * 256 : PAD + (ph + 1) * 256].bitcast(E5X4),
                    scales=sca[:, ph * 256 : (ph + 1) * 256],
                    in_=gt[n][:, ph * 2 * NB : (ph + 1) * 2 * NB],
                )
            gq[n] = (cod, sca)

        def passes(n, h, positions=range(NPOS)):
            cod, sca = gq[n]
            if positions[0] == 0:
                bank[(n, h)] = psum_m.tile([P, NB], F32, name="mx")
            for p in positions:
                nc.tensor.matmul_mx(
                    out=bank[(n, h)][:],
                    lhsT=cod[:, PAD + p * P : PAD + (p + 1) * P].bitcast(E5X4),
                    lhsT_scale=sca[:, p * P : (p + 1) * P],
                    rhs=wcod[(p, h)][:].bitcast(E4X4),
                    rhs_scale=wsca[(p, h)][:],
                    start=(p == 0),
                    stop=(p == NPOS - 1),
                )

        def evacuate(n, h, channels=16, first=0, on_vector=False):
            if h == 0:
                acc[n] = acc_pool.tile([P, OUTC], F32, name="acc")
            lo = h * HC + first * IH * IW
            dst = acc[n][:, lo : lo + channels * IH * IW].rearrange("q (c s) -> q c s", c=channels)
            src = bank[(n, h)][:, FIRST : FIRST + HC].rearrange("q (s c) -> q c s", c=16)[:, first : first + channels, :]
            if on_vector:
                nc.vector.tensor_copy(out=dst, in_=src)
            else:
                nc.scalar.copy(out=dst, in_=src)

        def o_rows(n):
            return ot_view[:, T_TILES.index(n), :] if n in T_TILES else ov_view[VT_TILES.index(n)]

        def store_part(n, lo, hi):
            nc.sync.dma_start(out=o_rows(n)[:, lo:hi], in_=acc[n][:, lo:hi])

        def store_one(n):
            nc.sync.dma_start(out=o_rows(n), in_=acc[n][:])

        def w_prepare(p, h, in_transpose_banks=False, warm=0):
            if in_transpose_banks:
                w_transpose(p, h, psum_t, "gt", warm)
            else:
                w_transpose(p, h, psum_m, "mx", warm)
            w_copy(p, h)

        load_w(0, 0)
        load_t(0)
        load_w(1, 0)
        load_w(2, 0)
        load_t(1)
        load_w(3, 0)
        for p in range(NPOS):
            load_w(p, 1)
        for n in range(2, NT):
            if n in T_TILES:
                load_t(n)
            else:
                load_v(n)

        w_prepare(0, 0, warm=4)
        w_prepare(1, 0, warm=2)
        w_prepare(2, 0, warm=0)
        deinterleave(0)
        transposes(0)
        regroup(0)
        w_quantise(0, 0)
        w_quantise(1, 0)
        w_prepare(3, 0, warm=2)
        deinterleave(1)
        w_quantise(2, 0)
        quantise(0)
        w_quantise(3, 0)
        transposes(1)
        regroup(1)
        w_prepare(0, 1, in_transpose_banks=True)
        w_prepare(1, 1, in_transpose_banks=True)
        quantise(1)
        passes(0, 0)
        w_quantise(0, 1)
        w_quantise(1, 1)
        w_prepare(2, 1)
        w_prepare(3, 1)
        deinterleave(2)
        passes(1, 0)
        evacuate(0, 0)
        evacuate(1, 0)
        transposes(2)
        regroup(2)
        w_quantise(2, 1)
        w_quantise(3, 1)
        passes(0, 1)
        evacuate(0, 1)
        store_one(0)
        deinterleave(3)
        transposes(3)
        quantise(2)
        regroup(3)
        passes(1, 1)
        evacuate(1, 1)
        store_one(1)
        deinterleave(4)
        for n in range(2, NT):
            if n + 2 in T_TILES:
                transposes(n + 2)
                regroup(n + 2)
            if n + 1 < NT:
                quantise(n + 1)
            if n + 2 in VT_TILES:
                v_transpose(n + 2)
            if n + 3 < NT and n + 3 not in S_TILES:
                deinterleave(n + 3)
            passes(n, 0)
            evacuate(n, 0)
            if n + S1 in S_TILES:
                deinterleave(n + S1, (0,))
            passes(n, 1)
            if n < NT - 1:
                evacuate(n, 1)
                store_one(n)
            if n + S1 in S_TILES:
                deinterleave(n + S1, (1,))
        store_part(NT - 1, 0, HC)
        for first in (0, 8):
            evacuate(NT - 1, 1, channels=8, first=first, on_vector=True)
            store_part(NT - 1, HC + first * IH * IW, HC + (first + 8) * IH * IW)
